import numpy as np
import ml_dtypes


def mxq(x, axis, fmt="e4m3"):
    dtype, down = {"e4m3": (ml_dtypes.float8_e4m3fn, 7), "e5m2": (ml_dtypes.float8_e5m2, 14)}[fmt]
    v = np.moveaxis(np.asarray(x, np.float32).astype(ml_dtypes.bfloat16).astype(np.float64), axis, -1)
    blocks = v.reshape(v.shape[:-1] + (-1, 32))
    amax = np.abs(blocks).max(-1, keepdims=True)
    byte = np.maximum(np.where(amax > 0, np.frexp(amax)[1] - 1 + 127, 0) - down, 1)
    scale = np.exp2(byte - 127.0)
    codes = (blocks / scale).astype(np.float32).astype(dtype).astype(np.float64)
    return np.moveaxis((codes * scale).reshape(v.shape), -1, axis)


WIDE = False


def mx_kscale(k):
    if not WIDE:
        return np.ones(k)
    levels = np.array([10, -10, 5, -5, 0])
    if k % 512:
        return np.exp2(np.random.permutation(np.resize(levels, k // 32))).repeat(32)
    a = np.empty((k // 512, 16))
    for p in range(k // 512):
        a[p, :8] = np.random.permutation(np.resize(levels, 8))
        for g in range(8):
            far = levels[np.abs(levels - a[p, g]) >= 10]
            a[p, g + 8] = far[np.random.randint(len(far))]
    return np.exp2(a.ravel()).repeat(32)


BF16 = ml_dtypes.bfloat16


def bf(x):
    return np.asarray(x, np.float32).astype(BF16)


def f64(x):
    return np.asarray(x).astype(np.float64)


B, C, CO, H, W = 2, 2048, 512, 24, 24
EPS = 1e-5
POOL_SIZES = (1, 2, 3, 6)
N = H * W


def bn_relu(y, scale, bias, mean, var):
    inv = scale / np.sqrt(var + EPS)
    return np.maximum((y - mean[None, :, None]) * inv[None, :, None] + bias[None, :, None], 0.0)


def pyramid_pool(f):
    feats = []
    for s in POOL_SIZES:
        p = f.reshape(B, CO, s, H // s, s, W // s).mean(axis=(3, 5))
        feats.append(p.reshape(B, CO, s * s))
    return np.concatenate(feats, axis=-1)


def draw0():
    s = mx_kscale(C)
    d = {}
    d["x"] = bf(np.random.standard_normal((B, C, H, W)) * s[None, :, None, None])
    for n in ("q", "k"):
        d["w" + n] = bf(np.random.standard_normal((CO, C)) * 0.5 / np.sqrt(C) / s[None, :])
        d[n + "_scale"] = bf(np.random.uniform(0.5, 1.5, CO))
        d[n + "_bias"] = bf(np.random.standard_normal(CO) * 0.1)
        d[n + "_mean"] = bf(np.random.standard_normal(CO) * 0.1)
        d[n + "_var"] = bf(np.random.uniform(0.5, 1.5, CO))
    return d


def core(x, wq, q_scale, q_bias, q_mean, q_var, wk, k_scale, k_bias, k_mean, k_var):
    xq = mxq(f64(x).reshape(B, C, N), 1, "e4m3")
    yq = mxq(f64(wq), 1, "e4m3") @ xq
    yk = mxq(f64(wk), 1, "e4m3") @ xq
    q = pyramid_pool(bn_relu(yq, f64(q_scale), f64(q_bias), f64(q_mean), f64(q_var)))
    k = pyramid_pool(bn_relu(yk, f64(k_scale), f64(k_bias), f64(k_mean), f64(k_var)))
    return q, k


def e4m3fn_bytes(y):
    return np.clip(np.asarray(y, np.float64), -448.0, 448.0).astype(np.float32).astype(ml_dtypes.float8_e4m3fn).view(np.uint8)


def e4m3fn_values(b):
    return np.asarray(b, np.uint8).view(ml_dtypes.float8_e4m3fn).astype(np.float64)


def setup_inputs():
    d = draw0()
    x0 = np.asarray(d['x']).astype(np.float64)
    s = (np.max(np.abs(x0), axis=(0, 2, 3), keepdims=True) / 448.0).astype(np.float32)
    out = {}
    for k, v in d.items():
        if k == 'x':
            out['x_bytes'] = e4m3fn_bytes(x0 / s.astype(np.float64))
            out['x_scale'] = s
        else:
            out[k] = v
    return out


def reference(x_bytes, x_scale, wq, q_scale, q_bias, q_mean, q_var, wk, k_scale, k_bias, k_mean, k_var):
    return core(e4m3fn_values(x_bytes) * x_scale.astype(np.float64), wq, q_scale, q_bias, q_mean, q_var, wk, k_scale, k_bias, k_mean, k_var)

@@ -1,0 +1,231 @@
+from contextlib import ExitStack
+
+import concourse.mybir as mybir
+from concourse.masks import make_identity
+
+F32 = mybir.dt.float32
+BF16 = mybir.dt.bfloat16
+U32 = mybir.dt.uint32
+U8 = mybir.dt.uint8
+FP8 = mybir.dt.float8_e4m3fn
+FP8X4 = mybir.dt.float8_e4m3fn_x4
+ACT = mybir.ActivationFunctionType
+ALU = mybir.AluOpType
+AX = mybir.AxisListType
+
+B, C, CO, HW = 2, 2048, 512, 576
+EPS = 1e-5
+P = 128
+G = 4
+NM = 8
+COLS = B * HW
+CHUNKS = ((0, 256), (256, 256), (512, 256), (768, 256), (1024, 128))
+POOL_AFTER = ((), ((0, 5),), ((5, 6),), ((6, 10),), ((10, 12),))
+V_EVAC = (0, 1, 2, 3)
+V_WIDEN = ((0, 2), (0, 3))
+
+FLOPS = 2 * 2 * CO * C * COLS
+
+
+def tile_guided_cam_module2_pa_kernel(
+    tc, x_bytes, x_scale, wq, q_scale, q_bias, q_mean, q_var,
+    wk, k_scale, k_bias, k_mean, k_var, out_0, out_1,
+):
+    nc = tc.nc
+    with ExitStack() as ctx:
+        const = ctx.enter_context(tc.tile_pool(name="const", bufs=1))
+        keep = ctx.enter_context(tc.tile_pool(name="keep", bufs=1))
+        xwp = ctx.enter_context(tc.tile_pool(name="xwp", bufs=2))
+        xgp = ctx.enter_context(tc.tile_pool(name="xgp", bufs=2))
+        wgp = ctx.enter_context(tc.tile_pool(name="wgp", bufs=3))
+        psum = ctx.enter_context(tc.psum_pool(name="psum", bufs=8))
+
+        ident = const.tile([P, P], F32, name="ident")
+        make_identity(nc, ident[:])
+
+        xs = const.tile([P, 4 * G], F32, name="xs")
+        nc.sync.dma_start(out=xs[:].rearrange("p (g t) -> p g t", t=4),
+                          in_=x_scale[0].rearrange("(g p t) a b -> p g (t a b)", p=P, t=4))
+        xb = {}
+        wraw = {}
+
+        def load_x(b, g):
+            xb[(b, g)] = keep.tile([P, 4, HW], U8, name="xb%d%d" % (b, g))
+            nc.sync.dma_start(
+                out=xb[(b, g)][:],
+                in_=x_bytes[b].rearrange("(g p t) h w -> g p t (h w)", p=P, t=4)[g])
+
+        def load_w(m):
+            w = wq if m < 4 else wk
+            wraw[m] = keep.tile([P, C], BF16, name="wraw%d" % m)
+            nc.sync.dma_start(out=wraw[m][:], in_=w.rearrange("(p m) k -> m p k", m=4)[m % 4])
+
+        load_x(0, 0)
+        load_x(0, 1)
+        load_w(0)
+        load_x(0, 2)
+        load_x(0, 3)
+        load_w(1)
+        bn_in = {}
+        for br, vecs in enumerate(((q_scale, q_bias, q_mean, q_var), (k_scale, k_bias, k_mean, k_var))):
+            for i, v in enumerate(vecs):
+                bn_in[(br, i)] = const.tile([P, 4], BF16, name="bn%d%d" % (br, i))
+                nc.sync.dma_start(out=bn_in[(br, i)][:], in_=v.rearrange("(p m) -> p m", m=4))
+        for m in range(2, NM):
+            load_w(m)
+        for g in range(G):
+            load_x(1, g)
+
+        warm = const.tile([P, 1], F32, name="warm")
+        nc.gpsimd.memset(warm[:], 0.0)
+        warm2 = const.tile([P, 1], F32, name="warm2")
+        nc.scalar.activation(out=warm2[:], in_=warm[:], func=ACT.Relu)
+
+        s16 = const.tile([P, NM], F32, name="s16")
+        b16 = const.tile([P, NM], F32, name="b16")
+        mean = const.tile([P, NM], F32, name="mean")
+        vare = const.tile([P, NM], F32, name="vare")
+        for br in range(2):
+            cols = slice(4 * br, 4 * br + 4)
+            nc.gpsimd.tensor_scalar(out=s16[:, cols], in0=bn_in[(br, 0)][:], scalar1=0.0625, scalar2=0.0, op0=ALU.mult, op1=ALU.add)
+            nc.gpsimd.tensor_scalar(out=b16[:, cols], in0=bn_in[(br, 1)][:], scalar1=0.0625, scalar2=0.0, op0=ALU.mult, op1=ALU.add)
+            nc.gpsimd.tensor_scalar(out=mean[:, cols], in0=bn_in[(br, 2)][:], scalar1=1.0, scalar2=0.0, op0=ALU.mult, op1=ALU.add)
+            nc.gpsimd.tensor_scalar(out=vare[:, cols], in0=bn_in[(br, 3)][:], scalar1=1.0, scalar2=EPS, op0=ALU.mult, op1=ALU.add)
+        expo = const.tile([P, NM], F32, name="expo")
+        nc.gpsimd.memset(expo[:], -0.5)
+        inv = const.tile([P, NM], F32, name="inv")
+        nc.gpsimd.tensor_tensor(out=inv[:], in0=vare[:], in1=expo[:], op=ALU.pow)
+        bn_a = const.tile([P, NM], F32, name="bn_a")
+        nc.gpsimd.tensor_tensor(out=bn_a[:], in0=s16[:], in1=inv[:], op=ALU.mult)
+        ma = const.tile([P, NM], F32, name="ma")
+        nc.gpsimd.tensor_tensor(out=ma[:], in0=mean[:], in1=bn_a[:], op=ALU.mult)
+        bn_b = const.tile([P, NM], F32, name="bn_b")
+        nc.gpsimd.tensor_tensor(out=bn_b[:], in0=b16[:], in1=ma[:], op=ALU.subtract)
+
+        fac = const.tile([P, NM, 14], F32, name="fac")
+        nc.gpsimd.memset(fac[:], 1.0)
+        nc.gpsimd.tensor_scalar(out=fac[:, :, 0:1], in0=fac[:, :, 0:1], scalar1=1.0 / 36.0, scalar2=0.0, op0=ALU.mult, op1=ALU.add)
+        nc.gpsimd.tensor_scalar(out=fac[:, :, 1:5], in0=fac[:, :, 1:5], scalar1=1.0 / 9.0, scalar2=0.0, op0=ALU.mult, op1=ALU.add)
+        nc.gpsimd.tensor_scalar(out=fac[:, :, 5:14], in0=fac[:, :, 5:14], scalar1=0.25, scalar2=0.0, op0=ALU.mult, op1=ALU.add)
+
+        res = const.tile([P, B, NM, 50], F32, name="res")
+        z = {}
+        for m in range(NM):
+            z[m] = keep.tile([P, COLS], F32, name="z%d" % m)
+
+        xc = {}
+        xsc = {}
+
+        def prep_x(c):
+            f0, width = CHUNKS[c]
+            xw = xwp.tile([P, G, 4, width], BF16, tag="xw")
+            f = f0
+            while f < f0 + width:
+                b, n0 = divmod(f, HW)
+                n1 = min(HW, n0 + f0 + width - f)
+                for g in range(G):
+                    for t in range(4):
+                        dst = xw[:, g, t, f - f0:f - f0 + n1 - n0]
+                        src = xb[(b, g)][:, t, n0:n1].bitcast(FP8)
+                        if (c, g) in V_WIDEN:
+                            nc.vector.tensor_scalar(out=dst, in0=src, scalar1=xs[:, 4 * g + t:4 * g + t + 1],
+                                                    scalar2=None, op0=ALU.mult)
+                        else:
+                            nc.scalar.activation(out=dst, in_=src, func=ACT.Copy,
+                                                 scale=xs[:, 4 * g + t:4 * g + t + 1])
+                f += n1 - n0
+            xg = xgp.tile([P, G * width * 4], BF16, tag="xg", align_bytes=64)
+            nc.vector.tensor_copy(out=xg[:].rearrange("p (g n t) -> p g n t", g=G, t=4),
+                                  in_=xw[:].rearrange("p g t n -> p g n t"))
+            xc[c] = keep.tile([P, G * width], U32, name="xc%d" % c, align_bytes=64)
+            xsc[c] = keep.tile([P, G * width], U8, name="xsc%d" % c, align_bytes=64)
+            nc.vector.quantize_mx(out=xc[c][:].bitcast(FP8X4), scales=xsc[c][:], in_=xg[:])
+
+        wc = {}
+        wsc = {}
+
+        def prep_w(m):
+            words = wraw[m][:].bitcast(F32)
+            wg = wgp.tile([P, G * P * 4], BF16, tag="wg", align_bytes=64)
+            wgw = wg[:].bitcast(F32)
+            for h in range(2):
+                pt = psum.tile([P, 512], F32, tag="bank")
+                for gg in range(2):
+                    g = 2 * h + gg
+                    for u in range(2):
+                        nc.tensor.transpose(pt[:, (2 * gg + u) * P:(2 * gg + u + 1) * P],
+                                            words[:, 256 * g + u:256 * (g + 1):2], ident[:])
+                dst = wgw[:, 512 * h:512 * (h + 1)].rearrange("p (g r u) -> p g r u", g=2, u=2)
+                src = pt[:].rearrange("p (g u r) -> p g r u", g=2, u=2)
+                if 2 * m + h in V_EVAC:
+                    nc.vector.tensor_copy(out=dst, in_=src)
+                else:
+                    nc.scalar.copy(out=dst, in_=src)
+            wc[m] = keep.tile([P, G * P], U32, name="wc%d" % m, align_bytes=64)
+            wsc[m] = keep.tile([P, G * P], U8, name="wsc%d" % m, align_bytes=64)
+            nc.vector.quantize_mx(out=wc[m][:].bitcast(FP8X4), scales=wsc[m][:], in_=wg[:])
+
+        acc = {}
+
+        def multiply(c, ms):
+            width = CHUNKS[c][1]
+            bank = psum.tile([P, 512], F32, tag="bank")
+            for i, m in enumerate(ms):
+                acc[(c, m)] = bank[:, i * width:(i + 1) * width]
+                for g in range(G):
+                    nc.tensor.matmul_mx(
+                        out=acc[(c, m)],
+                        lhsT=wc[m][:, g * P:(g + 1) * P].bitcast(FP8X4),
+                        lhsT_scale=wsc[m][:, g * P:(g + 1) * P],
+                        rhs=xc[c][:, g * width:(g + 1) * width].bitcast(FP8X4),
+                        rhs_scale=xsc[c][:, g * width:(g + 1) * width],
+                        start=(g == 0), stop=(g == G - 1))
+
+        def epilogue(c, m):
+            f0, width = CHUNKS[c]
+            nc.scalar.activation(out=z[m][:, f0:f0 + width], in_=acc[(c, m)], func=ACT.Relu,
+                                 bias=bn_b[:, m:m + 1], scale=bn_a[:, m:m + 1])
+            for r0, r1 in POOL_AFTER[c]:
+                b = r0 // 6
+                nc.vector.tensor_reduce(
+                    out=res[:, b, m, 14 + 6 * (r0 - 6 * b):14 + 6 * (r1 - 6 * b)].rearrange("p (r w) -> p r w", w=6),
+                    in_=z[m][:, 96 * r0:96 * r1].rearrange("p (r i w j) -> p r w i j", i=4, w=6, j=4),
+                    axis=AX.XY, op=ALU.add)
+
+        def coarse_levels(b):
+            fine = res[:, b, :, 14:50]
+            t3 = const.tile([P, NM, 18], F32, name="t3_%d" % b)
+            t2 = const.tile([P, NM, 12], F32, name="t2_%d" % b)
+            nc.vector.tensor_reduce(out=t3[:], in_=fine.rearrange("p x (q d) -> p x q d", d=2), axis=AX.X, op=ALU.add)
+            nc.vector.tensor_reduce(out=t2[:], in_=fine.rearrange("p x (q d) -> p x q d", d=3), axis=AX.X, op=ALU.add)
+            nc.vector.tensor_reduce(out=res[:, b, :, 5:14].rearrange("p x (i j) -> p x i j", j=3),
+                                    in_=t3[:].rearrange("p x (i d j) -> p x i j d", d=2, j=3), axis=AX.X, op=ALU.add)
+            nc.vector.tensor_reduce(out=res[:, b, :, 1:5].rearrange("p x (i j) -> p x i j", j=2),
+                                    in_=t2[:].rearrange("p x (i d j) -> p x i j d", d=3, j=2), axis=AX.X, op=ALU.add)
+            nc.vector.tensor_reduce(out=res[:, b, :, 0:1], in_=res[:, b, :, 1:5], axis=AX.X, op=ALU.add)
+            nc.vector.tensor_tensor(out=res[:, b, :, 0:14], in0=res[:, b, :, 0:14], in1=fac[:], op=ALU.mult)
+            for br, o in enumerate((out_0, out_1)):
+                eng = nc.sync if br == 0 else nc.scalar
+                eng.dma_start(out=o[b].rearrange("(p m) j -> p (m j)", m=4),
+                              in_=res[:, b, 4 * br:4 * br + 4, :].rearrange("p m j -> p (m j)"))
+
+        prep_x(0)
+        for j in range(4):
+            prep_w(2 * j)
+            prep_w(2 * j + 1)
+            multiply(0, (2 * j, 2 * j + 1))
+        for c in range(1, 5):
+            prep_x(c)
+            if c < 4:
+                for j in range(4):
+                    multiply(c, (2 * j, 2 * j + 1))
+            else:
+                for j in range(2):
+                    multiply(c, tuple(range(4 * j, 4 * j + 4)))
+            for m in range(NM):
+                epilogue(c - 1, m)
+            if c == 3:
+                coarse_levels(0)
+        for m in range(NM):
+            epilogue(4, m)
+        coarse_levels(1)

@@ -20,9 +20,12 @@ G = 4
 NM = 8
 COLS = B * HW
 CHUNKS = ((0, 256), (256, 256), (512, 256), (768, 256), (1024, 128))
-POOL_AFTER = ((), ((0, 5),), ((5, 6),), ((6, 10),), ((10, 12),))
-V_EVAC = (0, 1, 2, 3)
-V_WIDEN = ((0, 2), (0, 3))
+NC = len(CHUNKS)
+PIECES = ((0, 2, 0), (2, 5, 1), (5, 6, 2), (6, 8, 2), (8, 10, 3), (10, 12, 4))
+S_EVAC2 = (5, 7)
+V_WIDEN = ((2, 3),)
+WARM = 3
+DUMMY_N = 256
 
 FLOPS = 2 * 2 * CO * C * COLS
 
@@ -35,13 +38,18 @@ def tile_guided_cam_module2_pa_kernel(
     with ExitStack() as ctx:
         const = ctx.enter_context(tc.tile_pool(name="const", bufs=1))
         keep = ctx.enter_context(tc.tile_pool(name="keep", bufs=1))
-        xwp = ctx.enter_context(tc.tile_pool(name="xwp", bufs=2))
+        xwp = ctx.enter_context(tc.tile_pool(name="xwp", bufs=3))
         xgp = ctx.enter_context(tc.tile_pool(name="xgp", bufs=2))
         wgp = ctx.enter_context(tc.tile_pool(name="wgp", bufs=3))
         psum = ctx.enter_context(tc.psum_pool(name="psum", bufs=8))
+        ctx.enter_context(tc.manual_schedule())
 
+        zeros = const.tile([P, DUMMY_N], F32, name="zeros")
+        nc.vector.memset(zeros[:], 0.0)
         ident = const.tile([P, P], F32, name="ident")
         make_identity(nc, ident[:])
+        warm = const.tile([P, 1], F32, name="warm")
+        nc.scalar.activation(out=warm[:], in_=zeros[:, 0:1], func=ACT.Relu)
 
         xs = const.tile([P, 4 * G], F32, name="xs")
         nc.sync.dma_start(out=xs[:].rearrange("p (g t) -> p g t", t=4),
@@ -60,39 +68,36 @@ def tile_guided_cam_module2_pa_kernel(
             wraw[m] = keep.tile([P, C], BF16, name="wraw%d" % m)
             nc.sync.dma_start(out=wraw[m][:], in_=w.rearrange("(p m) k -> m p k", m=4)[m % 4])
 
-        load_x(0, 0)
-        load_x(0, 1)
-        load_w(0)
-        load_x(0, 2)
-        load_x(0, 3)
-        load_w(1)
+        for g in range(G):
+            load_x(0, g)
+            load_w(g)
         bn_in = {}
         for br, vecs in enumerate(((q_scale, q_bias, q_mean, q_var), (k_scale, k_bias, k_mean, k_var))):
             for i, v in enumerate(vecs):
                 bn_in[(br, i)] = const.tile([P, 4], BF16, name="bn%d%d" % (br, i))
                 nc.sync.dma_start(out=bn_in[(br, i)][:], in_=v.rearrange("(p m) -> p m", m=4))
-        for m in range(2, NM):
+        for m in range(4, NM):
             load_w(m)
         for g in range(G):
             load_x(1, g)
-
-        warm = const.tile([P, 1], F32, name="warm")
-        nc.gpsimd.memset(warm[:], 0.0)
-        warm2 = const.tile([P, 1], F32, name="warm2")
-        nc.scalar.activation(out=warm2[:], in_=warm[:], func=ACT.Relu)
 
         s16 = const.tile([P, NM], F32, name="s16")
         b16 = const.tile([P, NM], F32, name="b16")
         mean = const.tile([P, NM], F32, name="mean")
         vare = const.tile([P, NM], F32, name="vare")
+        expo = const.tile([P, NM], F32, name="expo")
+        nc.gpsimd.memset(expo[:], -0.5)
+        fac = const.tile([P, NM, 14], F32, name="fac")
+        nc.gpsimd.memset(fac[:], 1.0)
+        nc.gpsimd.tensor_scalar(out=fac[:, :, 0:1], in0=fac[:, :, 0:1], scalar1=1.0 / 36.0, scalar2=0.0, op0=ALU.mult, op1=ALU.add)
+        nc.gpsimd.tensor_scalar(out=fac[:, :, 1:5], in0=fac[:, :, 1:5], scalar1=1.0 / 9.0, scalar2=0.0, op0=ALU.mult, op1=ALU.add)
+        nc.gpsimd.tensor_scalar(out=fac[:, :, 5:14], in0=fac[:, :, 5:14], scalar1=0.25, scalar2=0.0, op0=ALU.mult, op1=ALU.add)
         for br in range(2):
             cols = slice(4 * br, 4 * br + 4)
             nc.gpsimd.tensor_scalar(out=s16[:, cols], in0=bn_in[(br, 0)][:], scalar1=0.0625, scalar2=0.0, op0=ALU.mult, op1=ALU.add)
             nc.gpsimd.tensor_scalar(out=b16[:, cols], in0=bn_in[(br, 1)][:], scalar1=0.0625, scalar2=0.0, op0=ALU.mult, op1=ALU.add)
             nc.gpsimd.tensor_scalar(out=mean[:, cols], in0=bn_in[(br, 2)][:], scalar1=1.0, scalar2=0.0, op0=ALU.mult, op1=ALU.add)
             nc.gpsimd.tensor_scalar(out=vare[:, cols], in0=bn_in[(br, 3)][:], scalar1=1.0, scalar2=EPS, op0=ALU.mult, op1=ALU.add)
-        expo = const.tile([P, NM], F32, name="expo")
-        nc.gpsimd.memset(expo[:], -0.5)
         inv = const.tile([P, NM], F32, name="inv")
         nc.gpsimd.tensor_tensor(out=inv[:], in0=vare[:], in1=expo[:], op=ALU.pow)
         bn_a = const.tile([P, NM], F32, name="bn_a")
@@ -102,70 +107,81 @@ def tile_guided_cam_module2_pa_kernel(
         bn_b = const.tile([P, NM], F32, name="bn_b")
         nc.gpsimd.tensor_tensor(out=bn_b[:], in0=b16[:], in1=ma[:], op=ALU.subtract)
 
-        fac = const.tile([P, NM, 14], F32, name="fac")
-        nc.gpsimd.memset(fac[:], 1.0)
-        nc.gpsimd.tensor_scalar(out=fac[:, :, 0:1], in0=fac[:, :, 0:1], scalar1=1.0 / 36.0, scalar2=0.0, op0=ALU.mult, op1=ALU.add)
-        nc.gpsimd.tensor_scalar(out=fac[:, :, 1:5], in0=fac[:, :, 1:5], scalar1=1.0 / 9.0, scalar2=0.0, op0=ALU.mult, op1=ALU.add)
-        nc.gpsimd.tensor_scalar(out=fac[:, :, 5:14], in0=fac[:, :, 5:14], scalar1=0.25, scalar2=0.0, op0=ALU.mult, op1=ALU.add)
-
         res = const.tile([P, B, NM, 50], F32, name="res")
         z = {}
         for m in range(NM):
             z[m] = keep.tile([P, COLS], F32, name="z%d" % m)
 
+        xw = {}
+        xg = {}
         xc = {}
         xsc = {}
+        wg = {}
+        wbank = {}
+        wc = {}
+        wsc = {}
+        acc = {}
 
-        def prep_x(c):
+        def dummy():
+            junk = psum.tile([P, 512], F32, tag="bank")
+            nc.tensor.matmul(out=junk[:, 0:DUMMY_N], lhsT=zeros[:, 0:P], rhs=zeros[:], start=True, stop=True)
+
+        def widen(c, g):
             f0, width = CHUNKS[c]
-            xw = xwp.tile([P, G, 4, width], BF16, tag="xw")
+            if g == 0:
+                xw[c] = xwp.tile([P, G, 4, width], BF16, name="xw", tag="xw")
             f = f0
             while f < f0 + width:
                 b, n0 = divmod(f, HW)
                 n1 = min(HW, n0 + f0 + width - f)
-                for g in range(G):
-                    for t in range(4):
-                        dst = xw[:, g, t, f - f0:f - f0 + n1 - n0]
-                        src = xb[(b, g)][:, t, n0:n1].bitcast(FP8)
-                        if (c, g) in V_WIDEN:
-                            nc.vector.tensor_scalar(out=dst, in0=src, scalar1=xs[:, 4 * g + t:4 * g + t + 1],
-                                                    scalar2=None, op0=ALU.mult)
-                        else:
-                            nc.scalar.activation(out=dst, in_=src, func=ACT.Copy,
-                                                 scale=xs[:, 4 * g + t:4 * g + t + 1])
+                for t in range(4):
+                    dst = xw[c][:, g, t, f - f0:f - f0 + n1 - n0]
+                    src = xb[(b, g)][:, t, n0:n1].bitcast(FP8)
+                    if (c, g) in V_WIDEN:
+                        nc.vector.tensor_scalar(out=dst, in0=src, scalar1=xs[:, 4 * g + t:4 * g + t + 1],
+                                                scalar2=None, op0=ALU.mult)
+                    else:
+                        nc.scalar.activation(out=dst, in_=src, func=ACT.Copy,
+                                             scale=xs[:, 4 * g + t:4 * g + t + 1])
                 f += n1 - n0
-            xg = xgp.tile([P, G * width * 4], BF16, tag="xg", align_bytes=64)
-            nc.vector.tensor_copy(out=xg[:].rearrange("p (g n t) -> p g n t", g=G, t=4),
-                                  in_=xw[:].rearrange("p g t n -> p g n t"))
+
+        def interleave(c, g):
+            width = CHUNKS[c][1]
+            if g == 0:
+                xg[c] = xgp.tile([P, G * width * 4], BF16, name="xg", tag="xg", align_bytes=64)
+            nc.vector.tensor_copy(
+                out=xg[c][:, g * width * 4:(g + 1) * width * 4].rearrange("p (n t) -> p n t", t=4),
+                in_=xw[c][:, g].rearrange("p t n -> p n t"))
+
+        def quantize_x(c):
+            width = CHUNKS[c][1]
             xc[c] = keep.tile([P, G * width], U32, name="xc%d" % c, align_bytes=64)
             xsc[c] = keep.tile([P, G * width], U8, name="xsc%d" % c, align_bytes=64)
-            nc.vector.quantize_mx(out=xc[c][:].bitcast(FP8X4), scales=xsc[c][:], in_=xg[:])
+            nc.vector.quantize_mx(out=xc[c][:].bitcast(FP8X4), scales=xsc[c][:], in_=xg[c][:])
 
-        wc = {}
-        wsc = {}
-
-        def prep_w(m):
+        def transposes(m, h):
             words = wraw[m][:].bitcast(F32)
-            wg = wgp.tile([P, G * P * 4], BF16, tag="wg", align_bytes=64)
-            wgw = wg[:].bitcast(F32)
-            for h in range(2):
-                pt = psum.tile([P, 512], F32, tag="bank")
-                for gg in range(2):
-                    g = 2 * h + gg
-                    for u in range(2):
-                        nc.tensor.transpose(pt[:, (2 * gg + u) * P:(2 * gg + u + 1) * P],
-                                            words[:, 256 * g + u:256 * (g + 1):2], ident[:])
-                dst = wgw[:, 512 * h:512 * (h + 1)].rearrange("p (g r u) -> p g r u", g=2, u=2)
-                src = pt[:].rearrange("p (g u r) -> p g r u", g=2, u=2)
-                if 2 * m + h in V_EVAC:
-                    nc.vector.tensor_copy(out=dst, in_=src)
-                else:
-                    nc.scalar.copy(out=dst, in_=src)
+            wbank[(m, h)] = psum.tile([P, 512], F32, name="wbank", tag="bank")
+            for gg in range(2):
+                g = 2 * h + gg
+                for u in range(2):
+                    nc.tensor.transpose(wbank[(m, h)][:, (2 * gg + u) * P:(2 * gg + u + 1) * P],
+                                        words[:, 256 * g + u:256 * (g + 1):2], ident[:])
+
+        def empty_w(m, h, eng):
+            if h == 0:
+                wg[m] = wgp.tile([P, G * P * 4], BF16, name="wg", tag="wg", align_bytes=64)
+            dst = wg[m][:].bitcast(F32)[:, 512 * h:512 * (h + 1)].rearrange("p (g r u) -> p g r u", g=2, u=2)
+            src = wbank[(m, h)][:].rearrange("p (g u r) -> p g r u", g=2, u=2)
+            if eng == "V":
+                nc.vector.tensor_copy(out=dst, in_=src)
+            else:
+                nc.scalar.copy(out=dst, in_=src)
+
+        def quantize_w(m):
             wc[m] = keep.tile([P, G * P], U32, name="wc%d" % m, align_bytes=64)
             wsc[m] = keep.tile([P, G * P], U8, name="wsc%d" % m, align_bytes=64)
-            nc.vector.quantize_mx(out=wc[m][:].bitcast(FP8X4), scales=wsc[m][:], in_=wg[:])
-
-        acc = {}
+            nc.vector.quantize_mx(out=wc[m][:].bitcast(FP8X4), scales=wsc[m][:], in_=wg[m][:])
 
         def multiply(c, ms):
             width = CHUNKS[c][1]
@@ -181,51 +197,74 @@ def tile_guided_cam_module2_pa_kernel(
                         rhs_scale=xsc[c][:, g * width:(g + 1) * width],
                         start=(g == 0), stop=(g == G - 1))
 
-        def epilogue(c, m):
+        def bn_relu(c, m):
             f0, width = CHUNKS[c]
             nc.scalar.activation(out=z[m][:, f0:f0 + width], in_=acc[(c, m)], func=ACT.Relu,
                                  bias=bn_b[:, m:m + 1], scale=bn_a[:, m:m + 1])
-            for r0, r1 in POOL_AFTER[c]:
-                b = r0 // 6
-                nc.vector.tensor_reduce(
-                    out=res[:, b, m, 14 + 6 * (r0 - 6 * b):14 + 6 * (r1 - 6 * b)].rearrange("p (r w) -> p r w", w=6),
-                    in_=z[m][:, 96 * r0:96 * r1].rearrange("p (r i w j) -> p r w i j", i=4, w=6, j=4),
-                    axis=AX.XY, op=ALU.add)
 
-        def coarse_levels(b):
-            fine = res[:, b, :, 14:50]
-            t3 = const.tile([P, NM, 18], F32, name="t3_%d" % b)
-            t2 = const.tile([P, NM, 12], F32, name="t2_%d" % b)
-            nc.vector.tensor_reduce(out=t3[:], in_=fine.rearrange("p x (q d) -> p x q d", d=2), axis=AX.X, op=ALU.add)
-            nc.vector.tensor_reduce(out=t2[:], in_=fine.rearrange("p x (q d) -> p x q d", d=3), axis=AX.X, op=ALU.add)
-            nc.vector.tensor_reduce(out=res[:, b, :, 5:14].rearrange("p x (i j) -> p x i j", j=3),
-                                    in_=t3[:].rearrange("p x (i d j) -> p x i j d", d=2, j=3), axis=AX.X, op=ALU.add)
-            nc.vector.tensor_reduce(out=res[:, b, :, 1:5].rearrange("p x (i j) -> p x i j", j=2),
-                                    in_=t2[:].rearrange("p x (i d j) -> p x i j d", d=3, j=2), axis=AX.X, op=ALU.add)
+        def pool(k, m):
+            r0, r1 = PIECES[k][0], PIECES[k][1]
+            b = r0 // 6
+            nc.vector.tensor_reduce(
+                out=res[:, b, m, 14 + 6 * (r0 - 6 * b):14 + 6 * (r1 - 6 * b)].rearrange("p (r w) -> p r w", w=6),
+                in_=z[m][:, 96 * r0:96 * r1].rearrange("p (r i w j) -> p r w i j", i=4, w=6, j=4),
+                axis=AX.XY, op=ALU.add)
+
+        def level(b, first, n, i):
+            d = 6 // n
+            nc.vector.tensor_reduce(
+                out=res[:, b, :, first + n * i:first + n * (i + 1)],
+                in_=res[:, b, :, 14 + 6 * d * i:14 + 6 * d * (i + 1)].rearrange("p x (d j e) -> p x j d e", d=d, e=d),
+                axis=AX.XY, op=ALU.add)
+
+        def finish(b):
             nc.vector.tensor_reduce(out=res[:, b, :, 0:1], in_=res[:, b, :, 1:5], axis=AX.X, op=ALU.add)
             nc.vector.tensor_tensor(out=res[:, b, :, 0:14], in0=res[:, b, :, 0:14], in1=fac[:], op=ALU.mult)
             for br, o in enumerate((out_0, out_1)):
-                eng = nc.sync if br == 0 else nc.scalar
-                eng.dma_start(out=o[b].rearrange("(p m) j -> p (m j)", m=4),
-                              in_=res[:, b, 4 * br:4 * br + 4, :].rearrange("p m j -> p (m j)"))
+                nc.sync.dma_start(out=o[b].rearrange("(p m) j -> p (m j)", m=4),
+                                  in_=res[:, b, 4 * br:4 * br + 4, :].rearrange("p m j -> p (m j)"))
 
-        prep_x(0)
-        for j in range(4):
-            prep_w(2 * j)
-            prep_w(2 * j + 1)
-            multiply(0, (2 * j, 2 * j + 1))
-        for c in range(1, 5):
-            prep_x(c)
-            if c < 4:
-                for j in range(4):
-                    multiply(c, (2 * j, 2 * j + 1))
-            else:
-                for j in range(2):
-                    multiply(c, tuple(range(4 * j, 4 * j + 4)))
-            for m in range(NM):
-                epilogue(c - 1, m)
-            if c == 3:
-                coarse_levels(0)
+        def coarse(c):
+            rows = [r for k in PIECES if k[2] == c for r in range(k[0], k[1])]
+            for b in range(B):
+                for n, first in ((3, 5), (2, 1)):
+                    d = 6 // n
+                    for i in range(n):
+                        if 6 * b + d * (i + 1) - 1 in rows:
+                            level(b, first, n, i)
+                if 6 * b + 5 in rows:
+                    finish(b)
+
+        for i in range(WARM):
+            dummy()
         for m in range(NM):
-            epilogue(4, m)
-        coarse_levels(1)
+            transposes(m, 0)
+            transposes(m, 1)
+            dummy()
+            c, g = divmod(m, 4)
+            widen(c, g)
+            empty_w(m, 0, "S")
+            interleave(c, g)
+            empty_w(m, 1, "S" if m in S_EVAC2 else "V")
+            quantize_w(m)
+            if g == 3:
+                quantize_x(c)
+        for c in range(NC):
+            per = 512 // CHUNKS[c][1]
+            for j in range(NM // per):
+                multiply(c, tuple(range(per * j, per * (j + 1))))
+            nxt = c + 2
+            if nxt < NC:
+                for g in range(G):
+                    widen(nxt, g)
+                    if g > 0:
+                        interleave(nxt, g - 1)
+                interleave(nxt, G - 1)
+            for m in range(NM):
+                bn_relu(c, m)
+                for k in range(len(PIECES)):
+                    if PIECES[k][2] == c:
+                        pool(k, m)
+                if m == 1 and nxt < NC:
+                    quantize_x(nxt)
+            coarse(c)

@@ -24,8 +24,9 @@ NC = len(CHUNKS)
 PIECES = ((0, 2, 0), (2, 5, 1), (5, 6, 2), (6, 8, 2), (8, 10, 3), (10, 12, 4))
 S_EVAC2 = (5, 7)
 V_WIDEN = ((2, 3),)
-WARM = 3
-DUMMY_N = 256
+WARM = 6
+WARM_N = 256
+DUMMY_N = 384
 
 FLOPS = 2 * 2 * CO * C * COLS
 
@@ -51,6 +52,11 @@ def tile_guided_cam_module2_pa_kernel(
         warm = const.tile([P, 1], F32, name="warm")
         nc.scalar.activation(out=warm[:], in_=zeros[:, 0:1], func=ACT.Relu)
 
+        bn_in = {}
+        for br, vecs in enumerate(((q_scale, q_bias, q_mean, q_var), (k_scale, k_bias, k_mean, k_var))):
+            for i, v in enumerate(vecs):
+                bn_in[(br, i)] = const.tile([P, 4], BF16, name="bn%d%d" % (br, i))
+                nc.gpsimd.dma_start(out=bn_in[(br, i)][:], in_=v.rearrange("(p m) -> p m", m=4))
         xs = const.tile([P, 4 * G], F32, name="xs")
         nc.sync.dma_start(out=xs[:].rearrange("p (g t) -> p g t", t=4),
                           in_=x_scale[0].rearrange("(g p t) a b -> p g (t a b)", p=P, t=4))
@@ -59,9 +65,12 @@ def tile_guided_cam_module2_pa_kernel(
 
         def load_x(b, g):
             xb[(b, g)] = keep.tile([P, 4, HW], U8, name="xb%d%d" % (b, g))
-            nc.sync.dma_start(
-                out=xb[(b, g)][:],
-                in_=x_bytes[b].rearrange("(g p t) h w -> g p t (h w)", p=P, t=4)[g])
+            src = x_bytes[b].rearrange("(g p t) h w -> g p t (h w)", p=P, t=4)[g]
+            if (b, g) == (0, 0):
+                nc.sync.dma_start(out=xb[(b, g)][:, 0:2], in_=src[:, 0:2])
+                nc.sync.dma_start(out=xb[(b, g)][:, 2:4], in_=src[:, 2:4])
+            else:
+                nc.sync.dma_start(out=xb[(b, g)][:], in_=src)
 
         def load_w(m):
             w = wq if m < 4 else wk
@@ -71,11 +80,6 @@ def tile_guided_cam_module2_pa_kernel(
         for g in range(G):
             load_x(0, g)
             load_w(g)
-        bn_in = {}
-        for br, vecs in enumerate(((q_scale, q_bias, q_mean, q_var), (k_scale, k_bias, k_mean, k_var))):
-            for i, v in enumerate(vecs):
-                bn_in[(br, i)] = const.tile([P, 4], BF16, name="bn%d%d" % (br, i))
-                nc.sync.dma_start(out=bn_in[(br, i)][:], in_=v.rearrange("(p m) -> p m", m=4))
         for m in range(4, NM):
             load_w(m)
         for g in range(G):
@@ -122,9 +126,9 @@ def tile_guided_cam_module2_pa_kernel(
         wsc = {}
         acc = {}
 
-        def dummy():
+        def dummy(n):
             junk = psum.tile([P, 512], F32, tag="bank")
-            nc.tensor.matmul(out=junk[:, 0:DUMMY_N], lhsT=zeros[:, 0:P], rhs=zeros[:], start=True, stop=True)
+            nc.tensor.matmul(out=junk[:, 0:n], lhsT=zeros[:, 0:P], rhs=zeros[:, 0:n], start=True, stop=True)
 
         def widen(c, g):
             f0, width = CHUNKS[c]
@@ -236,16 +240,16 @@ def tile_guided_cam_module2_pa_kernel(
                     finish(b)
 
         for i in range(WARM):
-            dummy()
+            dummy(WARM_N)
         for m in range(NM):
             transposes(m, 0)
             transposes(m, 1)
-            dummy()
+            dummy(DUMMY_N)
             c, g = divmod(m, 4)
             widen(c, g)
             empty_w(m, 0, "S")
-            interleave(c, g)
             empty_w(m, 1, "S" if m in S_EVAC2 else "V")
+            interleave(c, g)
             quantize_w(m)
             if g == 3:
                 quantize_x(c)

@@ -24,9 +24,8 @@ NC = len(CHUNKS)
 PIECES = ((0, 2, 0), (2, 5, 1), (5, 6, 2), (6, 8, 2), (8, 10, 3), (10, 12, 4))
 S_EVAC2 = (5, 7)
 V_WIDEN = ((2, 3),)
-WARM = 6
-WARM_N = 256
-DUMMY_N = 384
+WARM = 3
+DUMMY_N = 256
 
 FLOPS = 2 * 2 * CO * C * COLS
 
@@ -52,11 +51,6 @@ def tile_guided_cam_module2_pa_kernel(
         warm = const.tile([P, 1], F32, name="warm")
         nc.scalar.activation(out=warm[:], in_=zeros[:, 0:1], func=ACT.Relu)
 
-        bn_in = {}
-        for br, vecs in enumerate(((q_scale, q_bias, q_mean, q_var), (k_scale, k_bias, k_mean, k_var))):
-            for i, v in enumerate(vecs):
-                bn_in[(br, i)] = const.tile([P, 4], BF16, name="bn%d%d" % (br, i))
-                nc.gpsimd.dma_start(out=bn_in[(br, i)][:], in_=v.rearrange("(p m) -> p m", m=4))
         xs = const.tile([P, 4 * G], F32, name="xs")
         nc.sync.dma_start(out=xs[:].rearrange("p (g t) -> p g t", t=4),
                           in_=x_scale[0].rearrange("(g p t) a b -> p g (t a b)", p=P, t=4))
@@ -65,12 +59,9 @@ def tile_guided_cam_module2_pa_kernel(
 
         def load_x(b, g):
             xb[(b, g)] = keep.tile([P, 4, HW], U8, name="xb%d%d" % (b, g))
-            src = x_bytes[b].rearrange("(g p t) h w -> g p t (h w)", p=P, t=4)[g]
-            if (b, g) == (0, 0):
-                nc.sync.dma_start(out=xb[(b, g)][:, 0:2], in_=src[:, 0:2])
-                nc.sync.dma_start(out=xb[(b, g)][:, 2:4], in_=src[:, 2:4])
-            else:
-                nc.sync.dma_start(out=xb[(b, g)][:], in_=src)
+            nc.sync.dma_start(
+                out=xb[(b, g)][:],
+                in_=x_bytes[b].rearrange("(g p t) h w -> g p t (h w)", p=P, t=4)[g])
 
         def load_w(m):
             w = wq if m < 4 else wk
@@ -80,6 +71,11 @@ def tile_guided_cam_module2_pa_kernel(
         for g in range(G):
             load_x(0, g)
             load_w(g)
+        bn_in = {}
+        for br, vecs in enumerate(((q_scale, q_bias, q_mean, q_var), (k_scale, k_bias, k_mean, k_var))):
+            for i, v in enumerate(vecs):
+                bn_in[(br, i)] = const.tile([P, 4], BF16, name="bn%d%d" % (br, i))
+                nc.sync.dma_start(out=bn_in[(br, i)][:], in_=v.rearrange("(p m) -> p m", m=4))
         for m in range(4, NM):
             load_w(m)
         for g in range(G):
@@ -126,9 +122,9 @@ def tile_guided_cam_module2_pa_kernel(
         wsc = {}
         acc = {}
 
-        def dummy(n):
+        def dummy():
             junk = psum.tile([P, 512], F32, tag="bank")
-            nc.tensor.matmul(out=junk[:, 0:n], lhsT=zeros[:, 0:P], rhs=zeros[:, 0:n], start=True, stop=True)
+            nc.tensor.matmul(out=junk[:, 0:DUMMY_N], lhsT=zeros[:, 0:P], rhs=zeros[:], start=True, stop=True)
 
         def widen(c, g):
             f0, width = CHUNKS[c]
@@ -154,8 +150,8 @@ def tile_guided_cam_module2_pa_kernel(
             if g == 0:
                 xg[c] = xgp.tile([P, G * width * 4], BF16, name="xg", tag="xg", align_bytes=64)
             nc.vector.tensor_copy(
-                out=xg[c][:, g * width * 4:(g + 1) * width * 4].rearrange("p (n t) -> p n t", t=4),
-                in_=xw[c][:, g].rearrange("p t n -> p n t"))
+                out=xg[c][:, g * width * 4:(g + 1) * width * 4].rearrange("p (n i t) -> p n t i", i=4, t=4),
+                in_=xw[c][:, g].rearrange("p t (n i) -> p n t i", i=4))
 
         def quantize_x(c):
             width = CHUNKS[c][1]
@@ -240,16 +236,16 @@ def tile_guided_cam_module2_pa_kernel(
                     finish(b)
 
         for i in range(WARM):
-            dummy(WARM_N)
+            dummy()
         for m in range(NM):
             transposes(m, 0)
             transposes(m, 1)
-            dummy(DUMMY_N)
+            dummy()
             c, g = divmod(m, 4)
             widen(c, g)
             empty_w(m, 0, "S")
-            empty_w(m, 1, "S" if m in S_EVAC2 else "V")
             interleave(c, g)
+            empty_w(m, 1, "S" if m in S_EVAC2 else "V")
             quantize_w(m)
             if g == 3:
                 quantize_x(c)

@@ -71,19 +71,15 @@ def tile_guided_cam_module2_pa_kernel(
         for g in range(G):
             load_x(0, g)
             load_w(g)
-        bn_in = {}
+        bn_in = const.tile([P, 8, 16], BF16, name="bn_in")
         for br, vecs in enumerate(((q_scale, q_bias, q_mean, q_var), (k_scale, k_bias, k_mean, k_var))):
             for i, v in enumerate(vecs):
-                bn_in[(br, i)] = const.tile([P, 4], BF16, name="bn%d%d" % (br, i))
-                nc.sync.dma_start(out=bn_in[(br, i)][:], in_=v.rearrange("(p m) -> p m", m=4))
+                nc.sync.dma_start(out=bn_in[:, 2 * i + br, 0:4], in_=v.rearrange("(p m) -> p m", m=4))
         for m in range(4, NM):
             load_w(m)
         for g in range(G):
             load_x(1, g)
 
-        s16 = const.tile([P, NM], F32, name="s16")
-        b16 = const.tile([P, NM], F32, name="b16")
-        mean = const.tile([P, NM], F32, name="mean")
         vare = const.tile([P, NM], F32, name="vare")
         expo = const.tile([P, NM], F32, name="expo")
         nc.gpsimd.memset(expo[:], -0.5)
@@ -92,20 +88,25 @@ def tile_guided_cam_module2_pa_kernel(
         nc.gpsimd.tensor_scalar(out=fac[:, :, 0:1], in0=fac[:, :, 0:1], scalar1=1.0 / 36.0, scalar2=0.0, op0=ALU.mult, op1=ALU.add)
         nc.gpsimd.tensor_scalar(out=fac[:, :, 1:5], in0=fac[:, :, 1:5], scalar1=1.0 / 9.0, scalar2=0.0, op0=ALU.mult, op1=ALU.add)
         nc.gpsimd.tensor_scalar(out=fac[:, :, 5:14], in0=fac[:, :, 5:14], scalar1=0.25, scalar2=0.0, op0=ALU.mult, op1=ALU.add)
-        for br in range(2):
-            cols = slice(4 * br, 4 * br + 4)
-            nc.gpsimd.tensor_scalar(out=s16[:, cols], in0=bn_in[(br, 0)][:], scalar1=0.0625, scalar2=0.0, op0=ALU.mult, op1=ALU.add)
-            nc.gpsimd.tensor_scalar(out=b16[:, cols], in0=bn_in[(br, 1)][:], scalar1=0.0625, scalar2=0.0, op0=ALU.mult, op1=ALU.add)
-            nc.gpsimd.tensor_scalar(out=mean[:, cols], in0=bn_in[(br, 2)][:], scalar1=1.0, scalar2=0.0, op0=ALU.mult, op1=ALU.add)
-            nc.gpsimd.tensor_scalar(out=vare[:, cols], in0=bn_in[(br, 3)][:], scalar1=1.0, scalar2=EPS, op0=ALU.mult, op1=ALU.add)
+        def both(t):
+            return t[:].rearrange("p (b m) -> p b m", b=2)
+
+        nc.gpsimd.tensor_scalar(out=both(vare), in0=bn_in[:, 6:8, 0:4], scalar1=1.0, scalar2=EPS, op0=ALU.mult, op1=ALU.add)
         inv = const.tile([P, NM], F32, name="inv")
         nc.gpsimd.tensor_tensor(out=inv[:], in0=vare[:], in1=expo[:], op=ALU.pow)
         bn_a = const.tile([P, NM], F32, name="bn_a")
-        nc.gpsimd.tensor_tensor(out=bn_a[:], in0=s16[:], in1=inv[:], op=ALU.mult)
         ma = const.tile([P, NM], F32, name="ma")
-        nc.gpsimd.tensor_tensor(out=ma[:], in0=mean[:], in1=bn_a[:], op=ALU.mult)
         bn_b = const.tile([P, NM], F32, name="bn_b")
-        nc.gpsimd.tensor_tensor(out=bn_b[:], in0=b16[:], in1=ma[:], op=ALU.subtract)
+
+        def bn_step(i):
+            if i == 0:
+                nc.vector.scalar_tensor_tensor(out=both(bn_a), in0=bn_in[:, 0:2, 0:4], scalar=0.0625, in1=both(inv),
+                                               op0=ALU.mult, op1=ALU.mult)
+            elif i == 1:
+                nc.vector.tensor_tensor(out=both(ma), in0=bn_in[:, 4:6, 0:4], in1=both(bn_a), op=ALU.mult)
+            else:
+                nc.vector.scalar_tensor_tensor(out=both(bn_b), in0=bn_in[:, 2:4, 0:4], scalar=0.0625, in1=both(ma),
+                                               op0=ALU.mult, op1=ALU.subtract)
 
         res = const.tile([P, B, NM, 50], F32, name="res")
         z = {}
@@ -217,8 +218,10 @@ def tile_guided_cam_module2_pa_kernel(
                 in_=res[:, b, :, 14 + 6 * d * i:14 + 6 * d * (i + 1)].rearrange("p x (d j e) -> p x j d e", d=d, e=d),
                 axis=AX.XY, op=ALU.add)
 
-        def finish(b):
+        def total(b):
             nc.vector.tensor_reduce(out=res[:, b, :, 0:1], in_=res[:, b, :, 1:5], axis=AX.X, op=ALU.add)
+
+        def finish(b):
             nc.vector.tensor_tensor(out=res[:, b, :, 0:14], in0=res[:, b, :, 0:14], in1=fac[:], op=ALU.mult)
             for br, o in enumerate((out_0, out_1)):
                 nc.sync.dma_start(out=o[b].rearrange("(p m) j -> p (m j)", m=4),
@@ -226,14 +229,17 @@ def tile_guided_cam_module2_pa_kernel(
 
         def coarse(c):
             rows = [r for k in PIECES if k[2] == c for r in range(k[0], k[1])]
+            steps = []
             for b in range(B):
-                for n, first in ((3, 5), (2, 1)):
+                for n, first in ((2, 1), (3, 5)):
                     d = 6 // n
                     for i in range(n):
                         if 6 * b + d * (i + 1) - 1 in rows:
-                            level(b, first, n, i)
+                            steps.append((level, (b, first, n, i)))
                 if 6 * b + 5 in rows:
-                    finish(b)
+                    steps.append((total, (b,)))
+                    steps.append((finish, (b,)))
+            return steps
 
         for i in range(WARM):
             dummy()
@@ -244,11 +250,14 @@ def tile_guided_cam_module2_pa_kernel(
             c, g = divmod(m, 4)
             widen(c, g)
             empty_w(m, 0, "S")
-            interleave(c, g)
             empty_w(m, 1, "S" if m in S_EVAC2 else "V")
+            interleave(c, g)
             quantize_w(m)
+            if m >= NM - 3:
+                bn_step(m - (NM - 3))
             if g == 3:
                 quantize_x(c)
+        small = []
         for c in range(NC):
             per = 512 // CHUNKS[c][1]
             for j in range(NM // per):
@@ -267,4 +276,10 @@ def tile_guided_cam_module2_pa_kernel(
                         pool(k, m)
                 if m == 1 and nxt < NC:
                     quantize_x(nxt)
-            coarse(c)
+                if small:
+                    step, args = small[0]
+                    small = small[1:]
+                    step(*args)
+            small = small + coarse(c)
+        for step, args in small:
+            step(*args)

@@ -23,7 +23,8 @@ CHUNKS = ((0, 256), (256, 256), (512, 256), (768, 256), (1024, 128))
 NC = len(CHUNKS)
 PIECES = ((0, 2, 0), (2, 5, 1), (5, 6, 2), (6, 8, 2), (8, 10, 3), (10, 12, 4))
 S_EVAC2 = (5, 7)
-V_WIDEN = ((2, 3),)
+V_WIDEN = ((0, 1), (0, 3))
+AHEAD = 3
 WARM = 3
 DUMMY_N = 256
 
@@ -38,8 +39,8 @@ def tile_guided_cam_module2_pa_kernel(
     with ExitStack() as ctx:
         const = ctx.enter_context(tc.tile_pool(name="const", bufs=1))
         keep = ctx.enter_context(tc.tile_pool(name="keep", bufs=1))
-        xwp = ctx.enter_context(tc.tile_pool(name="xwp", bufs=3))
-        xgp = ctx.enter_context(tc.tile_pool(name="xgp", bufs=2))
+        xwp = ctx.enter_context(tc.tile_pool(name="xwp", bufs=4))
+        xgp = ctx.enter_context(tc.tile_pool(name="xgp", bufs=3))
         wgp = ctx.enter_context(tc.tile_pool(name="wgp", bufs=3))
         psum = ctx.enter_context(tc.psum_pool(name="psum", bufs=8))
         ctx.enter_context(tc.manual_schedule())
@@ -70,14 +71,14 @@ def tile_guided_cam_module2_pa_kernel(
 
         for g in range(G):
             load_x(0, g)
-            load_w(g)
+        for m in range(4):
+            load_w(m)
         bn_in = const.tile([P, 8, 16], BF16, name="bn_in")
         for br, vecs in enumerate(((q_scale, q_bias, q_mean, q_var), (k_scale, k_bias, k_mean, k_var))):
             for i, v in enumerate(vecs):
                 nc.sync.dma_start(out=bn_in[:, 2 * i + br, 0:4], in_=v.rearrange("(p m) -> p m", m=4))
-        for m in range(4, NM):
-            load_w(m)
         for g in range(G):
+            load_w(4 + g)
             load_x(1, g)
 
         vare = const.tile([P, NM], F32, name="vare")
@@ -211,23 +212,26 @@ def tile_guided_cam_module2_pa_kernel(
                 in_=z[m][:, 96 * r0:96 * r1].rearrange("p (r i w j) -> p r w i j", i=4, w=6, j=4),
                 axis=AX.XY, op=ALU.add)
 
-        def level(b, first, n, i):
+        def level(b, first, n, i, brs):
             d = 6 // n
+            ms = slice(4 * brs[0], 4 * brs[-1] + 4)
             nc.vector.tensor_reduce(
-                out=res[:, b, :, first + n * i:first + n * (i + 1)],
-                in_=res[:, b, :, 14 + 6 * d * i:14 + 6 * d * (i + 1)].rearrange("p x (d j e) -> p x j d e", d=d, e=d),
+                out=res[:, b, ms, first + n * i:first + n * (i + 1)],
+                in_=res[:, b, ms, 14 + 6 * d * i:14 + 6 * d * (i + 1)].rearrange("p x (d j e) -> p x j d e", d=d, e=d),
                 axis=AX.XY, op=ALU.add)
 
-        def total(b):
-            nc.vector.tensor_reduce(out=res[:, b, :, 0:1], in_=res[:, b, :, 1:5], axis=AX.X, op=ALU.add)
+        def total(b, brs):
+            ms = slice(4 * brs[0], 4 * brs[-1] + 4)
+            nc.vector.tensor_reduce(out=res[:, b, ms, 0:1], in_=res[:, b, ms, 1:5], axis=AX.X, op=ALU.add)
 
-        def finish(b):
-            nc.vector.tensor_tensor(out=res[:, b, :, 0:14], in0=res[:, b, :, 0:14], in1=fac[:], op=ALU.mult)
-            for br, o in enumerate((out_0, out_1)):
-                nc.sync.dma_start(out=o[b].rearrange("(p m) j -> p (m j)", m=4),
+        def finish(b, brs):
+            ms = slice(4 * brs[0], 4 * brs[-1] + 4)
+            nc.vector.tensor_tensor(out=res[:, b, ms, 0:14], in0=res[:, b, ms, 0:14], in1=fac[:, ms, :], op=ALU.mult)
+            for br in brs:
+                nc.sync.dma_start(out=(out_0, out_1)[br][b].rearrange("(p m) j -> p (m j)", m=4),
                                   in_=res[:, b, 4 * br:4 * br + 4, :].rearrange("p m j -> p (m j)"))
 
-        def coarse(c):
+        def coarse(c, brs):
             rows = [r for k in PIECES if k[2] == c for r in range(k[0], k[1])]
             steps = []
             for b in range(B):
@@ -235,22 +239,28 @@ def tile_guided_cam_module2_pa_kernel(
                     d = 6 // n
                     for i in range(n):
                         if 6 * b + d * (i + 1) - 1 in rows:
-                            steps.append((level, (b, first, n, i)))
+                            steps.append((level, (b, first, n, i, brs)))
                 if 6 * b + 5 in rows:
-                    steps.append((total, (b,)))
-                    steps.append((finish, (b,)))
+                    steps.append((total, (b, brs)))
+                    steps.append((finish, (b, brs)))
             return steps
 
         for i in range(WARM):
             dummy()
+        for g in range(G):
+            widen(0, g)
+            if g > 0:
+                interleave(0, g - 1)
+        interleave(0, G - 1)
         for m in range(NM):
             transposes(m, 0)
             transposes(m, 1)
-            dummy()
-            c, g = divmod(m, 4)
+            c, g = 1 + m // 4, m % 4
             widen(c, g)
             empty_w(m, 0, "S")
             empty_w(m, 1, "S" if m in S_EVAC2 else "V")
+            if m == 0:
+                quantize_x(0)
             interleave(c, g)
             quantize_w(m)
             if m >= NM - 3:
@@ -262,7 +272,7 @@ def tile_guided_cam_module2_pa_kernel(
             per = 512 // CHUNKS[c][1]
             for j in range(NM // per):
                 multiply(c, tuple(range(per * j, per * (j + 1))))
-            nxt = c + 2
+            nxt = c + AHEAD
             if nxt < NC:
                 for g in range(G):
                     widen(nxt, g)
@@ -280,6 +290,8 @@ def tile_guided_cam_module2_pa_kernel(
                     step, args = small[0]
                     small = small[1:]
                     step(*args)
-            small = small + coarse(c)
+                if c == NC - 1 and m == 3:
+                    small = small + coarse(c, (0,))
+            small = small + (coarse(c, (0, 1)) if c < NC - 1 else coarse(c, (1,)))
         for step, args in small:
             step(*args)

@@ -23,7 +23,10 @@ CHUNKS = ((0, 256), (256, 256), (512, 256), (768, 256), (1024, 128))
 NC = len(CHUNKS)
 PIECES = ((0, 2, 0), (2, 5, 1), (5, 6, 2), (6, 8, 2), (8, 10, 3), (10, 12, 4))
 S_EVAC2 = (5, 7)
-V_WIDEN = ((0, 1), (0, 3))
+V_WIDEN = ((0, 1), (0, 3), (3, 3))
+G_TILES = (4, 5, 6, 7)
+G_PIECES = ((2, 5, 1), (5, 8, 2), (8, 10, 3))
+G_ROW0 = 2
 AHEAD = 3
 WARM = 3
 DUMMY_N = 256
@@ -113,6 +116,9 @@ def tile_guided_cam_module2_pa_kernel(
         z = {}
         for m in range(NM):
             z[m] = keep.tile([P, COLS], F32, name="z%d" % m)
+        half = {}
+        for m in G_TILES:
+            half[m] = keep.tile([P, 48 * 8], F32, name="half%d" % m)
 
         xw = {}
         xg = {}
@@ -212,6 +218,18 @@ def tile_guided_cam_module2_pa_kernel(
                 in_=z[m][:, 96 * r0:96 * r1].rearrange("p (r i w j) -> p r w i j", i=4, w=6, j=4),
                 axis=AX.XY, op=ALU.add)
 
+        def halve(r0, r1, m):
+            rows = z[m][:, 96 * r0:96 * r1].rearrange("p (r h q) -> p r h q", h=2, q=48)
+            nc.gpsimd.tensor_tensor(out=half[m][:, 48 * (r0 - G_ROW0):48 * (r1 - G_ROW0)].rearrange("p (r q) -> p r q", q=48),
+                                    in0=rows[:, :, 0, :], in1=rows[:, :, 1, :], op=ALU.add)
+
+        def pool_half(r0, r1, m):
+            b = r0 // 6
+            nc.vector.tensor_reduce(
+                out=res[:, b, m, 14 + 6 * (r0 - 6 * b):14 + 6 * (r1 - 6 * b)].rearrange("p (r w) -> p r w", w=6),
+                in_=half[m][:, 48 * (r0 - G_ROW0):48 * (r1 - G_ROW0)].rearrange("p (r i w j) -> p r w i j", i=2, w=6, j=4),
+                axis=AX.XY, op=ALU.add)
+
         def level(b, first, n, i, brs):
             d = 6 // n
             ms = slice(4 * brs[0], 4 * brs[-1] + 4)
@@ -231,8 +249,7 @@ def tile_guided_cam_module2_pa_kernel(
                 nc.sync.dma_start(out=(out_0, out_1)[br][b].rearrange("(p m) j -> p (m j)", m=4),
                                   in_=res[:, b, 4 * br:4 * br + 4, :].rearrange("p m j -> p (m j)"))
 
-        def coarse(c, brs):
-            rows = [r for k in PIECES if k[2] == c for r in range(k[0], k[1])]
+        def coarse(rows, brs):
             steps = []
             for b in range(B):
                 for n, first in ((2, 1), (3, 5)):
@@ -255,6 +272,8 @@ def tile_guided_cam_module2_pa_kernel(
         for m in range(NM):
             transposes(m, 0)
             transposes(m, 1)
+            if m >= NM - 3 and m < NM - 1:
+                multiply(0, (2 * (m - (NM - 3)), 2 * (m - (NM - 3)) + 1))
             c, g = 1 + m // 4, m % 4
             widen(c, g)
             empty_w(m, 0, "S")
@@ -267,10 +286,15 @@ def tile_guided_cam_module2_pa_kernel(
                 bn_step(m - (NM - 3))
             if g == 3:
                 quantize_x(c)
+        multiply(1, (0, 1))
+        multiply(1, (2, 3))
+        for j in (2, 3):
+            multiply(0, (2 * j, 2 * j + 1))
+            multiply(1, (2 * j, 2 * j + 1))
         small = []
         for c in range(NC):
             per = 512 // CHUNKS[c][1]
-            for j in range(NM // per):
+            for j in range(NM // per if c >= 2 else 0):
                 multiply(c, tuple(range(per * j, per * (j + 1))))
             nxt = c + AHEAD
             if nxt < NC:
@@ -279,11 +303,22 @@ def tile_guided_cam_module2_pa_kernel(
                     if g > 0:
                         interleave(nxt, g - 1)
                 interleave(nxt, G - 1)
+            for r0, r1, cg in G_PIECES:
+                if cg == c - 1:
+                    for m in G_TILES:
+                        for k in PIECES:
+                            if r0 <= k[0] and k[1] <= r1:
+                                pool_half(k[0], k[1], m)
+                    small = small + coarse(list(range(r0, r1)), (0, 1))
             for m in range(NM):
                 bn_relu(c, m)
                 for k in range(len(PIECES)):
-                    if PIECES[k][2] == c:
+                    if PIECES[k][2] == c and (m not in G_TILES or not G_ROW0 <= PIECES[k][0] < 10):
                         pool(k, m)
+                if m in G_TILES:
+                    for r0, r1, cg in G_PIECES:
+                        if cg == c:
+                            halve(r0, r1, m)
                 if m == 1 and nxt < NC:
                     quantize_x(nxt)
                 if small:
@@ -291,7 +326,9 @@ def tile_guided_cam_module2_pa_kernel(
                     small = small[1:]
                     step(*args)
                 if c == NC - 1 and m == 3:
-                    small = small + coarse(c, (0,))
-            small = small + (coarse(c, (0, 1)) if c < NC - 1 else coarse(c, (1,)))
+                    small = small + coarse([10, 11], (0,))
+            if c == 0:
+                small = small + coarse([0, 1], (0, 1))
+        small = small + coarse([10, 11], (1,))
         for step, args in small:
             step(*args)

@@ -22,7 +22,7 @@ COLS = B * HW
 CHUNKS = ((0, 256), (256, 256), (512, 256), (768, 256), (1024, 128))
 NC = len(CHUNKS)
 PIECES = ((0, 2, 0), (2, 5, 1), (5, 6, 2), (6, 8, 2), (8, 10, 3), (10, 12, 4))
-S_EVAC2 = (5, 7)
+S_EVAC2 = (1, 3, 5, 7)
 V_WIDEN = ((0, 1), (0, 3), (3, 3))
 G_TILES = (4, 5, 6, 7)
 G_PIECES = ((2, 5, 1), (5, 8, 2), (8, 10, 3))
@@ -72,17 +72,24 @@ def tile_guided_cam_module2_pa_kernel(
             wraw[m] = keep.tile([P, C], BF16, name="wraw%d" % m)
             nc.sync.dma_start(out=wraw[m][:], in_=w.rearrange("(p m) k -> m p k", m=4)[m % 4])
 
+        bn_in = const.tile([P, 8, 16], BF16, name="bn_in")
+        bn_vecs = (q_scale, k_scale, q_bias, k_bias, q_mean, k_mean, q_var, k_var)
+
+        def load_bn(i):
+            nc.sync.dma_start(out=bn_in[:, i, 0:4], in_=bn_vecs[i].rearrange("(p m) -> p m", m=4))
+
         for g in range(G):
             load_x(0, g)
         for m in range(4):
             load_w(m)
-        bn_in = const.tile([P, 8, 16], BF16, name="bn_in")
-        for br, vecs in enumerate(((q_scale, q_bias, q_mean, q_var), (k_scale, k_bias, k_mean, k_var))):
-            for i, v in enumerate(vecs):
-                nc.sync.dma_start(out=bn_in[:, 2 * i + br, 0:4], in_=v.rearrange("(p m) -> p m", m=4))
+            load_bn((6, 7, 0, 1)[m])
         for g in range(G):
             load_w(4 + g)
+            if g < 2:
+                load_bn(4 + g)
             load_x(1, g)
+            if g < 2:
+                load_bn(2 + g)
 
         vare = const.tile([P, NM], F32, name="vare")
         expo = const.tile([P, NM], F32, name="expo")

@@ -55,9 +55,13 @@ def tile_guided_cam_module2_pa_kernel(
         warm = const.tile([P, 1], F32, name="warm")
         nc.scalar.activation(out=warm[:], in_=zeros[:, 0:1], func=ACT.Relu)
 
-        xs = const.tile([P, 4 * G], F32, name="xs")
-        nc.sync.dma_start(out=xs[:].rearrange("p (g t) -> p g t", t=4),
-                          in_=x_scale[0].rearrange("(g p t) a b -> p g (t a b)", p=P, t=4))
+        xs = const.tile([P, G, 8], F32, name="xs")
+        scales = x_scale[0].rearrange("(g p t) a b -> p g (t a b)", p=P, t=4)
+
+        def load_scales(g0, g1):
+            nc.sync.dma_start(out=xs[:, g0:g1, 0:4], in_=scales[:, g0:g1, :])
+
+        load_scales(0, 1)
         xb = {}
         wraw = {}
 
@@ -80,6 +84,8 @@ def tile_guided_cam_module2_pa_kernel(
 
         for g in range(G):
             load_x(0, g)
+            if g == 0:
+                load_scales(1, G)
         for m in range(4):
             load_w(m)
             load_bn((6, 7, 0, 1)[m])
@@ -153,11 +159,11 @@ def tile_guided_cam_module2_pa_kernel(
                     dst = xw[c][:, g, t, f - f0:f - f0 + n1 - n0]
                     src = xb[(b, g)][:, t, n0:n1].bitcast(FP8)
                     if (c, g) in V_WIDEN:
-                        nc.vector.tensor_scalar(out=dst, in0=src, scalar1=xs[:, 4 * g + t:4 * g + t + 1],
+                        nc.vector.tensor_scalar(out=dst, in0=src, scalar1=xs[:, g, t:t + 1],
                                                 scalar2=None, op0=ALU.mult)
                     else:
                         nc.scalar.activation(out=dst, in_=src, func=ACT.Copy,
-                                             scale=xs[:, 4 * g + t:4 * g + t + 1])
+                                             scale=xs[:, g, t:t + 1])
                 f += n1 - n0
 
         def interleave(c, g):

@@ -21,13 +21,13 @@ NM = 8
 COLS = B * HW
 CHUNKS = ((0, 256), (256, 256), (512, 256), (768, 256), (1024, 128))
 NC = len(CHUNKS)
-PIECES = ((0, 2, 0), (2, 5, 1), (5, 6, 2), (6, 8, 2), (8, 10, 3), (10, 12, 4))
-S_EVAC2 = (1, 3, 5, 7)
-V_WIDEN = ((0, 1), (0, 3), (3, 3))
+PIECES = ((0, 5, 1), (5, 6, 2), (6, 8, 2), (8, 10, 3), (10, 12, 4))
+S_EVAC2 = (0, 1, 2, 3, 4, 5, 6, 7)
+UNITS = ((0, 256), (256, 320), (576, 192), (768, 256), (1024, 128))
+V_WIDEN = ((0, 1), (0, 3), (1, 1), (1, 3), (3, 3))
 G_TILES = (4, 5, 6, 7)
-G_PIECES = ((2, 5, 1), (5, 8, 2), (8, 10, 3))
-G_ROW0 = 2
-AHEAD = 3
+G_PIECES = ((0, 5, 1), (5, 8, 2), (8, 10, 3))
+G_ROW0 = 0
 WARM = 3
 DUMMY_N = 256
 
@@ -42,7 +42,7 @@ def tile_guided_cam_module2_pa_kernel(
     with ExitStack() as ctx:
         const = ctx.enter_context(tc.tile_pool(name="const", bufs=1))
         keep = ctx.enter_context(tc.tile_pool(name="keep", bufs=1))
-        xwp = ctx.enter_context(tc.tile_pool(name="xwp", bufs=4))
+        xwp = ctx.enter_context(tc.tile_pool(name="xwp", bufs=1))
         xgp = ctx.enter_context(tc.tile_pool(name="xgp", bufs=3))
         wgp = ctx.enter_context(tc.tile_pool(name="wgp", bufs=3))
         psum = ctx.enter_context(tc.psum_pool(name="psum", bufs=8))
@@ -131,7 +131,7 @@ def tile_guided_cam_module2_pa_kernel(
             z[m] = keep.tile([P, COLS], F32, name="z%d" % m)
         half = {}
         for m in G_TILES:
-            half[m] = keep.tile([P, 48 * 8], F32, name="half%d" % m)
+            half[m] = keep.tile([P, 48 * 10], F32, name="half%d" % m)
 
         xw = {}
         xg = {}
@@ -142,37 +142,38 @@ def tile_guided_cam_module2_pa_kernel(
         wc = {}
         wsc = {}
         acc = {}
+        pair = {}
 
         def dummy():
             junk = psum.tile([P, 512], F32, tag="bank")
             nc.tensor.matmul(out=junk[:, 0:DUMMY_N], lhsT=zeros[:, 0:P], rhs=zeros[:], start=True, stop=True)
 
         def widen(c, g):
-            f0, width = CHUNKS[c]
+            f0, width = UNITS[c]
             if g == 0:
-                xw[c] = xwp.tile([P, G, 4, width], BF16, name="xw", tag="xw")
-            f = f0
-            while f < f0 + width:
-                b, n0 = divmod(f, HW)
-                n1 = min(HW, n0 + f0 + width - f)
-                for t in range(4):
-                    dst = xw[c][:, g, t, f - f0:f - f0 + n1 - n0]
-                    src = xb[(b, g)][:, t, n0:n1].bitcast(FP8)
-                    if (c, g) in V_WIDEN:
-                        nc.vector.tensor_scalar(out=dst, in0=src, scalar1=xs[:, g, t:t + 1],
-                                                scalar2=None, op0=ALU.mult)
-                    else:
-                        nc.scalar.activation(out=dst, in_=src, func=ACT.Copy,
-                                             scale=xs[:, g, t:t + 1])
-                f += n1 - n0
+                xw[c] = xwp.tile([P, G, 4, width], BF16, name="xw%d" % c, bufs=1)
+            b, n0 = divmod(f0, HW)
+            for t in range(4):
+                dst = xw[c][:, g, t, :]
+                src = xb[(b, g)][:, t, n0:n0 + width].bitcast(FP8)
+                if (c, g) in V_WIDEN:
+                    nc.vector.tensor_scalar(out=dst, in0=src, scalar1=xs[:, g, t:t + 1],
+                                            scalar2=None, op0=ALU.mult)
+                else:
+                    nc.scalar.activation(out=dst, in_=src, func=ACT.Copy,
+                                         scale=xs[:, g, t:t + 1])
 
         def interleave(c, g):
-            width = CHUNKS[c][1]
+            f0, width = CHUNKS[c]
             if g == 0:
                 xg[c] = xgp.tile([P, G * width * 4], BF16, name="xg", tag="xg", align_bytes=64)
-            nc.vector.tensor_copy(
-                out=xg[c][:, g * width * 4:(g + 1) * width * 4].rearrange("p (n i t) -> p n t i", i=4, t=4),
-                in_=xw[c][:, g].rearrange("p t (n i) -> p n t i", i=4))
+            for u, (u0, uw) in enumerate(UNITS):
+                a, b = max(f0, u0), min(f0 + width, u0 + uw)
+                if a < b:
+                    base = g * width * 4
+                    nc.vector.tensor_copy(
+                        out=xg[c][:, base + 4 * (a - f0):base + 4 * (b - f0)].rearrange("p (n i t) -> p n t i", i=4, t=4),
+                        in_=xw[u][:, g, :, a - u0:b - u0].rearrange("p t (n i) -> p n t i", i=4))
 
         def quantize_x(c):
             width = CHUNKS[c][1]
@@ -206,9 +207,15 @@ def tile_guided_cam_module2_pa_kernel(
 
         def multiply(c, ms):
             width = CHUNKS[c][1]
-            bank = psum.tile([P, 512], F32, tag="bank")
+            if c >= 2:
+                bank = psum.tile([P, 512], F32, tag="bank")
             for i, m in enumerate(ms):
-                acc[(c, m)] = bank[:, i * width:(i + 1) * width]
+                if c >= 2:
+                    acc[(c, m)] = bank[:, i * width:(i + 1) * width]
+                else:
+                    if m not in pair:
+                        pair[m] = psum.tile([P, 512], F32, name="pair", tag="bank")
+                    acc[(c, m)] = pair[m][:, c * width:(c + 1) * width]
                 for g in range(G):
                     nc.tensor.matmul_mx(
                         out=acc[(c, m)],
@@ -219,8 +226,8 @@ def tile_guided_cam_module2_pa_kernel(
                         start=(g == 0), stop=(g == G - 1))
 
         def bn_relu(c, m):
-            f0, width = CHUNKS[c]
-            nc.scalar.activation(out=z[m][:, f0:f0 + width], in_=acc[(c, m)], func=ACT.Relu,
+            f0, width = CHUNKS[c] if c >= 2 else (0, 512)
+            nc.scalar.activation(out=z[m][:, f0:f0 + width], in_=acc[(c, m)] if c >= 2 else pair[m][:], func=ACT.Relu,
                                  bias=bn_b[:, m:m + 1], scale=bn_a[:, m:m + 1])
 
         def pool(k, m):
@@ -305,17 +312,15 @@ def tile_guided_cam_module2_pa_kernel(
             multiply(0, (2 * j, 2 * j + 1))
             multiply(1, (2 * j, 2 * j + 1))
         small = []
-        for c in range(NC):
+        for g in range(G):
+            widen(3, g)
+            if g > 0:
+                interleave(3, g - 1)
+        interleave(3, G - 1)
+        for c in range(1, NC):
             per = 512 // CHUNKS[c][1]
             for j in range(NM // per if c >= 2 else 0):
                 multiply(c, tuple(range(per * j, per * (j + 1))))
-            nxt = c + AHEAD
-            if nxt < NC:
-                for g in range(G):
-                    widen(nxt, g)
-                    if g > 0:
-                        interleave(nxt, g - 1)
-                interleave(nxt, G - 1)
             for r0, r1, cg in G_PIECES:
                 if cg == c - 1:
                     for m in G_TILES:
@@ -332,16 +337,22 @@ def tile_guided_cam_module2_pa_kernel(
                     for r0, r1, cg in G_PIECES:
                         if cg == c:
                             halve(r0, r1, m)
-                if m == 1 and nxt < NC:
-                    quantize_x(nxt)
+                if c == 1 and m == 1:
+                    quantize_x(3)
                 if small:
                     step, args = small[0]
                     small = small[1:]
                     step(*args)
                 if c == NC - 1 and m == 3:
                     small = small + coarse([10, 11], (0,))
-            if c == 0:
-                small = small + coarse([0, 1], (0, 1))
+                if c == 1 and m == 1:
+                    for g in range(G):
+                        widen(4, g)
+                        if g > 0:
+                            interleave(4, g - 1)
+                    interleave(4, G - 1)
+            if c == 1:
+                quantize_x(4)
         small = small + coarse([10, 11], (1,))
         for step, args in small:
             step(*args)

@@ -24,8 +24,9 @@ NC = len(CHUNKS)
 PIECES = ((0, 5, 1), (5, 6, 2), (6, 8, 2), (8, 10, 3), (10, 12, 4))
 S_EVAC2 = (0, 1, 2, 3, 4, 5, 6, 7)
 UNITS = ((0, 256), (256, 320), (576, 192), (768, 256), (1024, 128))
-V_WIDEN = ((0, 1), (0, 3), (1, 1), (1, 3), (3, 3))
-G_TILES = (4, 5, 6, 7)
+V_WIDEN = ((1, 1), (1, 3), (3, 3))
+G_SETS = ((), (4, 5, 6, 7), (4, 5, 6, 7))
+G_TILES = tuple(sorted(set(G_SETS[0] + G_SETS[1] + G_SETS[2])))
 G_PIECES = ((0, 5, 1), (5, 8, 2), (8, 10, 3))
 G_ROW0 = 0
 WARM = 3
@@ -67,9 +68,10 @@ def tile_guided_cam_module2_pa_kernel(
 
         def load_x(b, g):
             xb[(b, g)] = keep.tile([P, 4, HW], U8, name="xb%d%d" % (b, g))
-            nc.sync.dma_start(
-                out=xb[(b, g)][:],
-                in_=x_bytes[b].rearrange("(g p t) h w -> g p t (h w)", p=P, t=4)[g])
+            for t0, t1 in (((0, 2), (2, 4)) if (b, g) == (0, 0) else ((0, 4),)):
+                nc.sync.dma_start(
+                    out=xb[(b, g)][:, t0:t1, :],
+                    in_=x_bytes[b].rearrange("(g p t) h w -> g p t (h w)", p=P, t=4)[g][:, t0:t1, :])
 
         def load_w(m):
             w = wq if m < 4 else wk
@@ -126,6 +128,12 @@ def tile_guided_cam_module2_pa_kernel(
                                                op0=ALU.mult, op1=ALU.subtract)
 
         res = const.tile([P, B, NM, 50], F32, name="res")
+        lev = {}
+        for n in (1, 2, 3):
+            lev[(n, 1)] = const.tile([P, NM, n * n], F32, name="lev%d" % n)
+        lev0 = const.tile([P, NM, 14], F32, name="lev0")
+        for n, first in ((1, 0), (2, 1), (3, 5)):
+            lev[(n, 0)] = lev0[:, :, first:first + n * n]
         z = {}
         for m in range(NM):
             z[m] = keep.tile([P, COLS], F32, name="z%d" % m)
@@ -156,7 +164,7 @@ def tile_guided_cam_module2_pa_kernel(
             for t in range(4):
                 dst = xw[c][:, g, t, :]
                 src = xb[(b, g)][:, t, n0:n0 + width].bitcast(FP8)
-                if (c, g) in V_WIDEN:
+                if (c, g) in V_WIDEN or (c == 0 and t >= 2):
                     nc.vector.tensor_scalar(out=dst, in0=src, scalar1=xs[:, g, t:t + 1],
                                             scalar2=None, op0=ALU.mult)
                 else:
@@ -250,37 +258,27 @@ def tile_guided_cam_module2_pa_kernel(
                 in_=half[m][:, 48 * (r0 - G_ROW0):48 * (r1 - G_ROW0)].rearrange("p (r i w j) -> p r w i j", i=2, w=6, j=4),
                 axis=AX.XY, op=ALU.add)
 
-        def level(b, first, n, i, brs):
+        def sums(b, n, i, ms):
             d = 6 // n
-            ms = slice(4 * brs[0], 4 * brs[-1] + 4)
-            nc.vector.tensor_reduce(
-                out=res[:, b, ms, first + n * i:first + n * (i + 1)],
-                in_=res[:, b, ms, 14 + 6 * d * i:14 + 6 * d * (i + 1)].rearrange("p x (d j e) -> p x j d e", d=d, e=d),
-                axis=AX.XY, op=ALU.add)
+            six = res[:, b, ms, 14 + 6 * d * i:14 + 6 * d * (i + 1)]
+            nc.vector.tensor_reduce(out=lev[(n, b)][:, ms, n * i:n * (i + 1)],
+                                    in_=six.rearrange("p x (d j e) -> p x j d e", d=d, e=d), axis=AX.XY, op=ALU.add)
 
-        def total(b, brs):
-            ms = slice(4 * brs[0], 4 * brs[-1] + 4)
-            nc.vector.tensor_reduce(out=res[:, b, ms, 0:1], in_=res[:, b, ms, 1:5], axis=AX.X, op=ALU.add)
+        def total(b, ms):
+            nc.vector.tensor_reduce(out=lev[(1, b)][:, ms, 0:1], in_=res[:, b, ms, 14:50], axis=AX.X, op=ALU.add)
 
-        def finish(b, brs):
-            ms = slice(4 * brs[0], 4 * brs[-1] + 4)
-            nc.vector.tensor_tensor(out=res[:, b, ms, 0:14], in0=res[:, b, ms, 0:14], in1=fac[:, ms, :], op=ALU.mult)
-            for br in brs:
-                nc.sync.dma_start(out=(out_0, out_1)[br][b].rearrange("(p m) j -> p (m j)", m=4),
-                                  in_=res[:, b, 4 * br:4 * br + 4, :].rearrange("p m j -> p (m j)"))
+        def means(b, ms, queue):
+            for n, first in ((2, 1), (3, 5), (1, 0)):
+                nc.scalar.activation(out=res[:, b, ms, first:first + n * n], in_=lev[(n, b)][:, ms, :], func=ACT.Copy, scale=n * n / 36.0)
+            for br in range(ms.start // 4, ms.stop // 4):
+                queue.dma_start(out=(out_0, out_1)[br][b].rearrange("(p m) j -> p (m j)", m=4),
+                                in_=res[:, b, 4 * br:4 * br + 4, :].rearrange("p m j -> p (m j)"))
 
-        def coarse(rows, brs):
-            steps = []
-            for b in range(B):
-                for n, first in ((2, 1), (3, 5)):
-                    d = 6 // n
-                    for i in range(n):
-                        if 6 * b + d * (i + 1) - 1 in rows:
-                            steps.append((level, (b, first, n, i, brs)))
-                if 6 * b + 5 in rows:
-                    steps.append((total, (b, brs)))
-                    steps.append((finish, (b, brs)))
-            return steps
+        def finish0():
+            nc.vector.tensor_tensor(out=res[:, 0, :, 0:14], in0=lev0[:], in1=fac[:], op=ALU.mult)
+            for br in range(2):
+                nc.sync.dma_start(out=(out_0, out_1)[br][0].rearrange("(p m) j -> p (m j)", m=4),
+                                  in_=res[:, 0, 4 * br:4 * br + 4, :].rearrange("p m j -> p (m j)"))
 
         for i in range(WARM):
             dummy()
@@ -297,62 +295,75 @@ def tile_guided_cam_module2_pa_kernel(
             c, g = 1 + m // 4, m % 4
             widen(c, g)
             empty_w(m, 0, "S")
-            empty_w(m, 1, "S" if m in S_EVAC2 else "V")
-            if m == 0:
+            empty_w(m, 1, "S")
+            if m == 1:
                 quantize_x(0)
-            interleave(c, g)
-            quantize_w(m)
+            if m > 0:
+                quantize_w(m - 1)
             if m >= NM - 3:
                 bn_step(m - (NM - 3))
-            if g == 3:
-                quantize_x(c)
+            interleave(c, g)
+            if m == 4:
+                quantize_x(1)
+        quantize_w(NM - 1)
+        for g in range(G):
+            widen(3, g)
+            if g == 0:
+                quantize_x(2)
+            if g > 0:
+                interleave(3, g - 1)
+        interleave(3, G - 1)
         multiply(1, (0, 1))
         multiply(1, (2, 3))
         for j in (2, 3):
             multiply(0, (2 * j, 2 * j + 1))
             multiply(1, (2 * j, 2 * j + 1))
-        small = []
-        for g in range(G):
-            widen(3, g)
-            if g > 0:
-                interleave(3, g - 1)
-        interleave(3, G - 1)
         for c in range(1, NC):
             per = 512 // CHUNKS[c][1]
             for j in range(NM // per if c >= 2 else 0):
                 multiply(c, tuple(range(per * j, per * (j + 1))))
-            for r0, r1, cg in G_PIECES:
+            for i, (r0, r1, cg) in enumerate(G_PIECES):
                 if cg == c - 1:
-                    for m in G_TILES:
+                    for m in G_SETS[i]:
                         for k in PIECES:
                             if r0 <= k[0] and k[1] <= r1:
                                 pool_half(k[0], k[1], m)
-                    small = small + coarse(list(range(r0, r1)), (0, 1))
+            if c == 3:
+                for n in (2, 3):
+                    for i in range(n):
+                        sums(0, n, i, slice(0, 8))
+                total(0, slice(0, 8))
+            if c == 4:
+                for n, i in ((2, 0), (3, 0), (3, 1)):
+                    sums(1, n, i, slice(0, 8))
             for m in range(NM):
                 bn_relu(c, m)
                 for k in range(len(PIECES)):
-                    if PIECES[k][2] == c and (m not in G_TILES or not G_ROW0 <= PIECES[k][0] < 10):
+                    if PIECES[k][2] == c and not any(m in G_SETS[i] and G_PIECES[i][0] <= PIECES[k][0] < G_PIECES[i][1] for i in range(3)):
                         pool(k, m)
-                if m in G_TILES:
-                    for r0, r1, cg in G_PIECES:
-                        if cg == c:
-                            halve(r0, r1, m)
-                if c == 1 and m == 1:
+                for i in range(3):
+                    if G_PIECES[i][2] == c and m in G_SETS[i]:
+                        halve(G_PIECES[i][0], G_PIECES[i][1], m)
+                if c == 1 and m == 0:
                     quantize_x(3)
-                if small:
-                    step, args = small[0]
-                    small = small[1:]
-                    step(*args)
-                if c == NC - 1 and m == 3:
-                    small = small + coarse([10, 11], (0,))
-                if c == 1 and m == 1:
+                if c == 1 and m == 3:
                     for g in range(G):
                         widen(4, g)
                         if g > 0:
                             interleave(4, g - 1)
                     interleave(4, G - 1)
-            if c == 1:
-                quantize_x(4)
-        small = small + coarse([10, 11], (1,))
-        for step, args in small:
-            step(*args)
+                if c == 1 and m == 3+1:
+                    quantize_x(4)
+                if c == 3 and m == 1:
+                    finish0()
+                if c == NC - 1 and m == 4:
+                    sums(1, 2, 1, slice(0, 4))
+                if c == NC - 1 and m == 5:
+                    sums(1, 3, 2, slice(0, 4))
+                if c == NC - 1 and m == 6:
+                    total(1, slice(0, 4))
+        sums(1, 2, 1, slice(4, 8))
+        sums(1, 3, 2, slice(4, 8))
+        total(1, slice(4, 8))
+        means(1, slice(0, 4), nc.sync)
+        means(1, slice(4, 8), nc.scalar)

@@ -53,9 +53,6 @@ def tile_guided_cam_module2_pa_kernel(
         nc.vector.memset(zeros[:], 0.0)
         ident = const.tile([P, P], F32, name="ident")
         make_identity(nc, ident[:])
-        warm = const.tile([P, 1], F32, name="warm")
-        nc.scalar.activation(out=warm[:], in_=zeros[:, 0:1], func=ACT.Relu)
-
         xs = const.tile([P, G, 8], F32, name="xs")
         scales = x_scale[0].rearrange("(g p t) a b -> p g (t a b)", p=P, t=4)
 
@@ -82,7 +79,12 @@ def tile_guided_cam_module2_pa_kernel(
         bn_vecs = (q_scale, k_scale, q_bias, k_bias, q_mean, k_mean, q_var, k_var)
 
         def load_bn(i):
-            nc.sync.dma_start(out=bn_in[:, i, 0:4], in_=bn_vecs[i].rearrange("(p m) -> p m", m=4))
+            (nc.scalar if i >= 6 else nc.sync).dma_start(out=bn_in[:, i, 0:4], in_=bn_vecs[i].rearrange("(p m) -> p m", m=4))
+
+        load_bn(6)
+        load_bn(7)
+        warm = const.tile([P, 1], F32, name="warm")
+        nc.scalar.activation(out=warm[:], in_=zeros[:, 0:1], func=ACT.Relu)
 
         for g in range(G):
             load_x(0, g)
@@ -90,7 +92,8 @@ def tile_guided_cam_module2_pa_kernel(
                 load_scales(1, G)
         for m in range(4):
             load_w(m)
-            load_bn((6, 7, 0, 1)[m])
+            if m >= 2:
+                load_bn(m - 2)
         for g in range(G):
             load_w(4 + g)
             if g < 2:
@@ -129,11 +132,11 @@ def tile_guided_cam_module2_pa_kernel(
 
         res = const.tile([P, B, NM, 50], F32, name="res")
         lev = {}
-        for n in (1, 2, 3):
-            lev[(n, 1)] = const.tile([P, NM, n * n], F32, name="lev%d" % n)
-        lev0 = const.tile([P, NM, 14], F32, name="lev0")
-        for n, first in ((1, 0), (2, 1), (3, 5)):
-            lev[(n, 0)] = lev0[:, :, first:first + n * n]
+        coarse = {}
+        for b in range(B):
+            coarse[b] = const.tile([P, NM, 14], F32, name="coarse%d" % b)
+            for n, first in ((1, 0), (2, 1), (3, 5)):
+                lev[(n, b)] = coarse[b][:, :, first:first + n * n]
         z = {}
         for m in range(NM):
             z[m] = keep.tile([P, COLS], F32, name="z%d" % m)
@@ -265,20 +268,14 @@ def tile_guided_cam_module2_pa_kernel(
                                     in_=six.rearrange("p x (d j e) -> p x j d e", d=d, e=d), axis=AX.XY, op=ALU.add)
 
         def total(b, ms):
-            nc.vector.tensor_reduce(out=lev[(1, b)][:, ms, 0:1], in_=res[:, b, ms, 14:50], axis=AX.X, op=ALU.add)
+            nc.vector.tensor_reduce(out=lev[(1, b)][:, ms, 0:1], in_=lev[(2, b)][:, ms, :], axis=AX.X, op=ALU.add)
 
-        def means(b, ms, queue):
-            for n, first in ((2, 1), (3, 5), (1, 0)):
-                nc.scalar.activation(out=res[:, b, ms, first:first + n * n], in_=lev[(n, b)][:, ms, :], func=ACT.Copy, scale=n * n / 36.0)
-            for br in range(ms.start // 4, ms.stop // 4):
-                queue.dma_start(out=(out_0, out_1)[br][b].rearrange("(p m) j -> p (m j)", m=4),
-                                in_=res[:, b, 4 * br:4 * br + 4, :].rearrange("p m j -> p (m j)"))
-
-        def finish0():
-            nc.vector.tensor_tensor(out=res[:, 0, :, 0:14], in0=lev0[:], in1=fac[:], op=ALU.mult)
-            for br in range(2):
-                nc.sync.dma_start(out=(out_0, out_1)[br][0].rearrange("(p m) j -> p (m j)", m=4),
-                                  in_=res[:, 0, 4 * br:4 * br + 4, :].rearrange("p m j -> p (m j)"))
+        def finish(b, brs):
+            ms = slice(4 * brs[0], 4 * brs[-1] + 4)
+            nc.vector.tensor_tensor(out=res[:, b, ms, 0:14], in0=coarse[b][:, ms, :], in1=fac[:, ms, :], op=ALU.mult)
+            for br in brs:
+                nc.sync.dma_start(out=(out_0, out_1)[br][b].rearrange("(p m) j -> p (m j)", m=4),
+                                  in_=res[:, b, 4 * br:4 * br + 4, :].rearrange("p m j -> p (m j)"))
 
         for i in range(WARM):
             dummy()
@@ -355,15 +352,15 @@ def tile_guided_cam_module2_pa_kernel(
                 if c == 1 and m == 3+1:
                     quantize_x(4)
                 if c == 3 and m == 1:
-                    finish0()
+                    finish(0, (0, 1))
                 if c == NC - 1 and m == 4:
                     sums(1, 2, 1, slice(0, 4))
                 if c == NC - 1 and m == 5:
                     sums(1, 3, 2, slice(0, 4))
                 if c == NC - 1 and m == 6:
                     total(1, slice(0, 4))
+        finish(1, (0,))
         sums(1, 2, 1, slice(4, 8))
         sums(1, 3, 2, slice(4, 8))
         total(1, slice(4, 8))
-        means(1, slice(0, 4), nc.sync)
-        means(1, slice(4, 8), nc.scalar)
+        finish(1, (1,))

@@ -24,8 +24,8 @@ NC = len(CHUNKS)
 PIECES = ((0, 5, 1), (5, 6, 2), (6, 8, 2), (8, 10, 3), (10, 12, 4))
 S_EVAC2 = (0, 1, 2, 3, 4, 5, 6, 7)
 UNITS = ((0, 256), (256, 320), (576, 192), (768, 256), (1024, 128))
-V_WIDEN = ((1, 1), (1, 3), (3, 3))
-G_SETS = ((), (4, 5, 6, 7), (4, 5, 6, 7))
+V_WIDEN = ((1, 1), (1, 3), (2, 3), (3, 3))
+G_SETS = ((), (2, 3, 4, 5), ())
 G_TILES = tuple(sorted(set(G_SETS[0] + G_SETS[1] + G_SETS[2])))
 G_PIECES = ((0, 5, 1), (5, 8, 2), (8, 10, 3))
 G_ROW0 = 0
@@ -277,6 +277,33 @@ def tile_guided_cam_module2_pa_kernel(
                 nc.sync.dma_start(out=(out_0, out_1)[br][b].rearrange("(p m) j -> p (m j)", m=4),
                                   in_=res[:, b, 4 * br:4 * br + 4, :].rearrange("p m j -> p (m j)"))
 
+        def gadd(out, in0, in1):
+            nc.gpsimd.tensor_tensor(out=out, in0=in0, in1=in1, op=ALU.add)
+
+        def coarse_gpsimd():
+            six = res[:, 0, :, 14:50]
+            r3 = six.rearrange("p m (i d w) -> p m i d w", i=3, d=2)
+            r2 = six.rearrange("p m (i d w) -> p m i d w", i=2, d=3)
+            t3 = const.tile([P, NM, 18], F32, name="t3")
+            t2 = const.tile([P, NM, 12], F32, name="t2")
+            u2 = const.tile([P, NM, 4], F32, name="u2")
+            v2 = const.tile([P, NM, 2], F32, name="v2")
+            t2v = t2[:].rearrange("p m (i w) -> p m i w", w=6)
+            gadd(t2v, r2[:, :, :, 0, :], r2[:, :, :, 1, :])
+            gadd(t3[:].rearrange("p m (i w) -> p m i w", w=6), r3[:, :, :, 0, :], r3[:, :, :, 1, :])
+            gadd(t2v, t2v, r2[:, :, :, 2, :])
+            c3 = t3[:].rearrange("p m (j e) -> p m j e", e=2)
+            gadd(lev[(3, 0)], c3[:, :, :, 0], c3[:, :, :, 1])
+            c2 = t2[:].rearrange("p m (j e) -> p m j e", e=3)
+            gadd(u2[:], c2[:, :, :, 0], c2[:, :, :, 1])
+            gadd(lev[(2, 0)], u2[:], c2[:, :, :, 2])
+            gadd(v2[:], coarse[0][:, :, 1:3], coarse[0][:, :, 3:5])
+            gadd(lev[(1, 0)], v2[:, :, 0:1], v2[:, :, 1:2])
+            nc.gpsimd.tensor_tensor(out=res[:, 0, :, 0:14], in0=coarse[0][:], in1=fac[:], op=ALU.mult)
+            for br in range(2):
+                nc.sync.dma_start(out=(out_0, out_1)[br][0].rearrange("(p m) j -> p (m j)", m=4),
+                                  in_=res[:, 0, 4 * br:4 * br + 4, :].rearrange("p m j -> p (m j)"))
+
         for i in range(WARM):
             dummy()
         for g in range(G):
@@ -326,10 +353,7 @@ def tile_guided_cam_module2_pa_kernel(
                             if r0 <= k[0] and k[1] <= r1:
                                 pool_half(k[0], k[1], m)
             if c == 3:
-                for n in (2, 3):
-                    for i in range(n):
-                        sums(0, n, i, slice(0, 8))
-                total(0, slice(0, 8))
+                coarse_gpsimd()
             if c == 4:
                 for n, i in ((2, 0), (3, 0), (3, 1)):
                     sums(1, n, i, slice(0, 8))
@@ -351,8 +375,6 @@ def tile_guided_cam_module2_pa_kernel(
                     interleave(4, G - 1)
                 if c == 1 and m == 3+1:
                     quantize_x(4)
-                if c == 3 and m == 1:
-                    finish(0, (0, 1))
                 if c == NC - 1 and m == 4:
                     sums(1, 2, 1, slice(0, 4))
                 if c == NC - 1 and m == 5:

@@ -19,16 +19,14 @@ P = 128
 G = 4
 NM = 8
 COLS = B * HW
+
 CHUNKS = ((0, 256), (256, 256), (512, 256), (768, 256), (1024, 128))
-NC = len(CHUNKS)
-PIECES = ((0, 5, 1), (5, 6, 2), (6, 8, 2), (8, 10, 3), (10, 12, 4))
-S_EVAC2 = (0, 1, 2, 3, 4, 5, 6, 7)
 UNITS = ((0, 256), (256, 320), (576, 192), (768, 256), (1024, 128))
 V_WIDEN = ((1, 1), (1, 3), (2, 3), (3, 3))
-G_SETS = ((), (2, 3, 4, 5), ())
-G_TILES = tuple(sorted(set(G_SETS[0] + G_SETS[1] + G_SETS[2])))
-G_PIECES = ((0, 5, 1), (5, 8, 2), (8, 10, 3))
-G_ROW0 = 0
+STAGES = ((0, 512), (512, 256), (768, 256), (1024, 128))
+STAGE_ROWS = ((0, 5), (5, 8), (8, 10), (10, 12))
+HALF_ROWS = (5, 8)
+HALF_TILES = (2, 3, 4, 5)
 WARM = 3
 DUMMY_N = 256
 
@@ -43,7 +41,6 @@ def tile_guided_cam_module2_pa_kernel(
     with ExitStack() as ctx:
         const = ctx.enter_context(tc.tile_pool(name="const", bufs=1))
         keep = ctx.enter_context(tc.tile_pool(name="keep", bufs=1))
-        xwp = ctx.enter_context(tc.tile_pool(name="xwp", bufs=1))
         xgp = ctx.enter_context(tc.tile_pool(name="xgp", bufs=3))
         wgp = ctx.enter_context(tc.tile_pool(name="wgp", bufs=3))
         psum = ctx.enter_context(tc.psum_pool(name="psum", bufs=8))
@@ -53,66 +50,67 @@ def tile_guided_cam_module2_pa_kernel(
         nc.vector.memset(zeros[:], 0.0)
         ident = const.tile([P, P], F32, name="ident")
         make_identity(nc, ident[:])
+
+        bn_in = const.tile([P, 8, 16], BF16, name="bn_in")
+        bn_vecs = (q_scale, k_scale, q_bias, k_bias, q_mean, k_mean, q_var, k_var)
+
+        def load_bn(i, queue):
+            queue.dma_start(out=bn_in[:, i, 0:4], in_=bn_vecs[i].rearrange("(p m) -> p m", m=4))
+
+        load_bn(6, nc.scalar)
+        load_bn(7, nc.scalar)
+        warm = const.tile([P, 1], F32, name="warm")
+        nc.scalar.activation(out=warm[:], in_=zeros[:, 0:1], func=ACT.Relu)
+
         xs = const.tile([P, G, 8], F32, name="xs")
         scales = x_scale[0].rearrange("(g p t) a b -> p g (t a b)", p=P, t=4)
 
         def load_scales(g0, g1):
             nc.sync.dma_start(out=xs[:, g0:g1, 0:4], in_=scales[:, g0:g1, :])
 
-        load_scales(0, 1)
         xb = {}
         wraw = {}
 
-        def load_x(b, g):
+        def load_x(b, g, halves):
             xb[(b, g)] = keep.tile([P, 4, HW], U8, name="xb%d%d" % (b, g))
-            for t0, t1 in (((0, 2), (2, 4)) if (b, g) == (0, 0) else ((0, 4),)):
-                nc.sync.dma_start(
-                    out=xb[(b, g)][:, t0:t1, :],
-                    in_=x_bytes[b].rearrange("(g p t) h w -> g p t (h w)", p=P, t=4)[g][:, t0:t1, :])
+            src = x_bytes[b].rearrange("(g p t) h w -> g p t (h w)", p=P, t=4)[g]
+            for t0, t1 in ((0, 2), (2, 4)) if halves else ((0, 4),):
+                nc.sync.dma_start(out=xb[(b, g)][:, t0:t1, :], in_=src[:, t0:t1, :])
 
         def load_w(m):
             w = wq if m < 4 else wk
             wraw[m] = keep.tile([P, C], BF16, name="wraw%d" % m)
             nc.sync.dma_start(out=wraw[m][:], in_=w.rearrange("(p m) k -> m p k", m=4)[m % 4])
 
-        bn_in = const.tile([P, 8, 16], BF16, name="bn_in")
-        bn_vecs = (q_scale, k_scale, q_bias, k_bias, q_mean, k_mean, q_var, k_var)
-
-        def load_bn(i):
-            (nc.scalar if i >= 6 else nc.sync).dma_start(out=bn_in[:, i, 0:4], in_=bn_vecs[i].rearrange("(p m) -> p m", m=4))
-
-        load_bn(6)
-        load_bn(7)
-        warm = const.tile([P, 1], F32, name="warm")
-        nc.scalar.activation(out=warm[:], in_=zeros[:, 0:1], func=ACT.Relu)
-
-        for g in range(G):
-            load_x(0, g)
-            if g == 0:
-                load_scales(1, G)
+        load_scales(0, 1)
+        load_x(0, 0, True)
+        load_scales(1, G)
+        for g in range(1, G):
+            load_x(0, g, False)
         for m in range(4):
             load_w(m)
             if m >= 2:
-                load_bn(m - 2)
+                load_bn(m - 2, nc.sync)
         for g in range(G):
             load_w(4 + g)
             if g < 2:
-                load_bn(4 + g)
-            load_x(1, g)
+                load_bn(4 + g, nc.sync)
+            load_x(1, g, False)
             if g < 2:
-                load_bn(2 + g)
+                load_bn(2 + g, nc.sync)
 
-        vare = const.tile([P, NM], F32, name="vare")
-        expo = const.tile([P, NM], F32, name="expo")
-        nc.gpsimd.memset(expo[:], -0.5)
         fac = const.tile([P, NM, 14], F32, name="fac")
         nc.gpsimd.memset(fac[:], 1.0)
-        nc.gpsimd.tensor_scalar(out=fac[:, :, 0:1], in0=fac[:, :, 0:1], scalar1=1.0 / 36.0, scalar2=0.0, op0=ALU.mult, op1=ALU.add)
-        nc.gpsimd.tensor_scalar(out=fac[:, :, 1:5], in0=fac[:, :, 1:5], scalar1=1.0 / 9.0, scalar2=0.0, op0=ALU.mult, op1=ALU.add)
-        nc.gpsimd.tensor_scalar(out=fac[:, :, 5:14], in0=fac[:, :, 5:14], scalar1=0.25, scalar2=0.0, op0=ALU.mult, op1=ALU.add)
+        for first, end, factor in ((0, 1, 1.0 / 36.0), (1, 5, 1.0 / 9.0), (5, 14, 0.25)):
+            nc.gpsimd.tensor_scalar(out=fac[:, :, first:end], in0=fac[:, :, first:end], scalar1=factor, scalar2=0.0,
+                                    op0=ALU.mult, op1=ALU.add)
+
         def both(t):
             return t[:].rearrange("p (b m) -> p b m", b=2)
 
+        expo = const.tile([P, NM], F32, name="expo")
+        nc.gpsimd.memset(expo[:], -0.5)
+        vare = const.tile([P, NM], F32, name="vare")
         nc.gpsimd.tensor_scalar(out=both(vare), in0=bn_in[:, 6:8, 0:4], scalar1=1.0, scalar2=EPS, op0=ALU.mult, op1=ALU.add)
         inv = const.tile([P, NM], F32, name="inv")
         nc.gpsimd.tensor_tensor(out=inv[:], in0=vare[:], in1=expo[:], op=ALU.pow)
@@ -131,18 +129,16 @@ def tile_guided_cam_module2_pa_kernel(
                                                op0=ALU.mult, op1=ALU.subtract)
 
         res = const.tile([P, B, NM, 50], F32, name="res")
-        lev = {}
         coarse = {}
         for b in range(B):
             coarse[b] = const.tile([P, NM, 14], F32, name="coarse%d" % b)
-            for n, first in ((1, 0), (2, 1), (3, 5)):
-                lev[(n, b)] = coarse[b][:, :, first:first + n * n]
+        FIRST = {1: 0, 2: 1, 3: 5}
         z = {}
+        half = {}
         for m in range(NM):
             z[m] = keep.tile([P, COLS], F32, name="z%d" % m)
-        half = {}
-        for m in G_TILES:
-            half[m] = keep.tile([P, 48 * 10], F32, name="half%d" % m)
+            if m in HALF_TILES:
+                half[m] = keep.tile([P, 48 * (HALF_ROWS[1] - HALF_ROWS[0])], F32, name="half%d" % m)
 
         xw = {}
         xg = {}
@@ -153,26 +149,24 @@ def tile_guided_cam_module2_pa_kernel(
         wc = {}
         wsc = {}
         acc = {}
-        pair = {}
+        sums_bank = {}
 
         def dummy():
-            junk = psum.tile([P, 512], F32, tag="bank")
+            junk = psum.tile([P, 512], F32, name="junk", tag="bank")
             nc.tensor.matmul(out=junk[:, 0:DUMMY_N], lhsT=zeros[:, 0:P], rhs=zeros[:], start=True, stop=True)
 
-        def widen(c, g):
-            f0, width = UNITS[c]
+        def widen(u, g):
+            f0, width = UNITS[u]
             if g == 0:
-                xw[c] = xwp.tile([P, G, 4, width], BF16, name="xw%d" % c, bufs=1)
+                xw[u] = keep.tile([P, G, 4, width], BF16, name="xw%d" % u)
             b, n0 = divmod(f0, HW)
             for t in range(4):
-                dst = xw[c][:, g, t, :]
+                dst = xw[u][:, g, t, :]
                 src = xb[(b, g)][:, t, n0:n0 + width].bitcast(FP8)
-                if (c, g) in V_WIDEN or (c == 0 and t >= 2):
-                    nc.vector.tensor_scalar(out=dst, in0=src, scalar1=xs[:, g, t:t + 1],
-                                            scalar2=None, op0=ALU.mult)
+                if (u, g) in V_WIDEN or (u == 0 and t >= 2):
+                    nc.vector.tensor_scalar(out=dst, in0=src, scalar1=xs[:, g, t:t + 1], scalar2=None, op0=ALU.mult)
                 else:
-                    nc.scalar.activation(out=dst, in_=src, func=ACT.Copy,
-                                         scale=xs[:, g, t:t + 1])
+                    nc.scalar.activation(out=dst, in_=src, func=ACT.Copy, scale=xs[:, g, t:t + 1])
 
         def interleave(c, g):
             f0, width = CHUNKS[c]
@@ -181,10 +175,14 @@ def tile_guided_cam_module2_pa_kernel(
             for u, (u0, uw) in enumerate(UNITS):
                 a, b = max(f0, u0), min(f0 + width, u0 + uw)
                 if a < b:
-                    base = g * width * 4
-                    nc.vector.tensor_copy(
-                        out=xg[c][:, base + 4 * (a - f0):base + 4 * (b - f0)].rearrange("p (n i t) -> p n t i", i=4, t=4),
-                        in_=xw[u][:, g, :, a - u0:b - u0].rearrange("p t (n i) -> p n t i", i=4))
+                    dst = xg[c][:, 4 * (g * width + a - f0):4 * (g * width + b - f0)]
+                    src = xw[u][:, g, :, a - u0:b - u0]
+                    if c == len(CHUNKS) - 1:
+                        nc.gpsimd.tensor_scalar(out=dst.rearrange("p (n t) -> p n t", t=4), in0=src.rearrange("p t n -> p n t"),
+                                                scalar1=1.0, scalar2=0.0, op0=ALU.mult, op1=ALU.add)
+                    else:
+                        nc.vector.tensor_copy(out=dst.rearrange("p (n i t) -> p n t i", i=4, t=4),
+                                              in_=src.rearrange("p t (n i) -> p n t i", i=4))
 
         def quantize_x(c):
             width = CHUNKS[c][1]
@@ -201,108 +199,109 @@ def tile_guided_cam_module2_pa_kernel(
                     nc.tensor.transpose(wbank[(m, h)][:, (2 * gg + u) * P:(2 * gg + u + 1) * P],
                                         words[:, 256 * g + u:256 * (g + 1):2], ident[:])
 
-        def empty_w(m, h, eng):
+        def empty_w(m, h):
             if h == 0:
                 wg[m] = wgp.tile([P, G * P * 4], BF16, name="wg", tag="wg", align_bytes=64)
-            dst = wg[m][:].bitcast(F32)[:, 512 * h:512 * (h + 1)].rearrange("p (g r u) -> p g r u", g=2, u=2)
-            src = wbank[(m, h)][:].rearrange("p (g u r) -> p g r u", g=2, u=2)
-            if eng == "V":
-                nc.vector.tensor_copy(out=dst, in_=src)
-            else:
-                nc.scalar.copy(out=dst, in_=src)
+            nc.scalar.copy(
+                out=wg[m][:].bitcast(F32)[:, 512 * h:512 * (h + 1)].rearrange("p (g r u) -> p g r u", g=2, u=2),
+                in_=wbank[(m, h)][:].rearrange("p (g u r) -> p g r u", g=2, u=2))
 
         def quantize_w(m):
             wc[m] = keep.tile([P, G * P], U32, name="wc%d" % m, align_bytes=64)
             wsc[m] = keep.tile([P, G * P], U8, name="wsc%d" % m, align_bytes=64)
             nc.vector.quantize_mx(out=wc[m][:].bitcast(FP8X4), scales=wsc[m][:], in_=wg[m][:])
 
-        def multiply(c, ms):
-            width = CHUNKS[c][1]
-            if c >= 2:
-                bank = psum.tile([P, 512], F32, tag="bank")
-            for i, m in enumerate(ms):
-                if c >= 2:
-                    acc[(c, m)] = bank[:, i * width:(i + 1) * width]
-                else:
-                    if m not in pair:
-                        pair[m] = psum.tile([P, 512], F32, name="pair", tag="bank")
-                    acc[(c, m)] = pair[m][:, c * width:(c + 1) * width]
-                for g in range(G):
-                    nc.tensor.matmul_mx(
-                        out=acc[(c, m)],
-                        lhsT=wc[m][:, g * P:(g + 1) * P].bitcast(FP8X4),
-                        lhsT_scale=wsc[m][:, g * P:(g + 1) * P],
-                        rhs=xc[c][:, g * width:(g + 1) * width].bitcast(FP8X4),
-                        rhs_scale=xsc[c][:, g * width:(g + 1) * width],
-                        start=(g == 0), stop=(g == G - 1))
+        def multiply(c, m):
+            f0, width = CHUNKS[c]
+            bank, col = (("pair", m), f0) if c < 2 else ((c, m * width // 512), m * width % 512)
+            if bank not in sums_bank:
+                sums_bank[bank] = psum.tile([P, 512], F32, name="sums", tag="bank")
+            acc[(c, m)] = sums_bank[bank][:, col:col + width]
+            for g in range(G):
+                nc.tensor.matmul_mx(
+                    out=acc[(c, m)],
+                    lhsT=wc[m][:, g * P:(g + 1) * P].bitcast(FP8X4),
+                    lhsT_scale=wsc[m][:, g * P:(g + 1) * P],
+                    rhs=xc[c][:, g * width:(g + 1) * width].bitcast(FP8X4),
+                    rhs_scale=xsc[c][:, g * width:(g + 1) * width],
+                    start=(g == 0), stop=(g == G - 1))
 
-        def bn_relu(c, m):
-            f0, width = CHUNKS[c] if c >= 2 else (0, 512)
-            nc.scalar.activation(out=z[m][:, f0:f0 + width], in_=acc[(c, m)] if c >= 2 else pair[m][:], func=ACT.Relu,
+        def bn_relu(s, m):
+            f0, width = STAGES[s]
+            src = sums_bank[("pair", m)][:] if s == 0 else acc[(s + 1, m)]
+            nc.scalar.activation(out=z[m][:, f0:f0 + width], in_=src, func=ACT.Relu,
                                  bias=bn_b[:, m:m + 1], scale=bn_a[:, m:m + 1])
 
-        def pool(k, m):
-            r0, r1 = PIECES[k][0], PIECES[k][1]
-            b = r0 // 6
-            nc.vector.tensor_reduce(
-                out=res[:, b, m, 14 + 6 * (r0 - 6 * b):14 + 6 * (r1 - 6 * b)].rearrange("p (r w) -> p r w", w=6),
-                in_=z[m][:, 96 * r0:96 * r1].rearrange("p (r i w j) -> p r w i j", i=4, w=6, j=4),
-                axis=AX.XY, op=ALU.add)
+        def by_batch(r0, r1):
+            return [(max(r0, 6 * b), min(r1, 6 * b + 6)) for b in range(B) if max(r0, 6 * b) < min(r1, 6 * b + 6)]
 
-        def halve(r0, r1, m):
-            rows = z[m][:, 96 * r0:96 * r1].rearrange("p (r h q) -> p r h q", h=2, q=48)
-            nc.gpsimd.tensor_tensor(out=half[m][:, 48 * (r0 - G_ROW0):48 * (r1 - G_ROW0)].rearrange("p (r q) -> p r q", q=48),
+        def means_6x6(r0, r1, m):
+            b = r0 // 6
+            return res[:, b, m, 14 + 6 * (r0 - 6 * b):14 + 6 * (r1 - 6 * b)].rearrange("p (r w) -> p r w", w=6)
+
+        def pool(r0, r1, m):
+            for a, e in by_batch(r0, r1):
+                nc.vector.tensor_reduce(out=means_6x6(a, e, m),
+                                        in_=z[m][:, 96 * a:96 * e].rearrange("p (r i w j) -> p r w i j", i=4, w=6, j=4),
+                                        axis=AX.XY, op=ALU.add)
+
+        def halve(m):
+            rows = z[m][:, 96 * HALF_ROWS[0]:96 * HALF_ROWS[1]].rearrange("p (r h q) -> p r h q", h=2, q=48)
+            nc.gpsimd.tensor_tensor(out=half[m][:].rearrange("p (r q) -> p r q", q=48),
                                     in0=rows[:, :, 0, :], in1=rows[:, :, 1, :], op=ALU.add)
 
-        def pool_half(r0, r1, m):
-            b = r0 // 6
+        def pool_half(m):
+            for a, e in by_batch(*HALF_ROWS):
+                src = half[m][:, 48 * (a - HALF_ROWS[0]):48 * (e - HALF_ROWS[0])]
+                nc.vector.tensor_reduce(out=means_6x6(a, e, m), in_=src.rearrange("p (r i w j) -> p r w i j", i=2, w=6, j=4),
+                                        axis=AX.XY, op=ALU.add)
+
+        def level(n, i, br):
+            d = 6 // n
+            ms = slice(4 * br, 4 * br + 4)
             nc.vector.tensor_reduce(
-                out=res[:, b, m, 14 + 6 * (r0 - 6 * b):14 + 6 * (r1 - 6 * b)].rearrange("p (r w) -> p r w", w=6),
-                in_=half[m][:, 48 * (r0 - G_ROW0):48 * (r1 - G_ROW0)].rearrange("p (r i w j) -> p r w i j", i=2, w=6, j=4),
+                out=coarse[1][:, ms, FIRST[n] + n * i:FIRST[n] + n * (i + 1)],
+                in_=res[:, 1, ms, 14 + 6 * d * i:14 + 6 * d * (i + 1)].rearrange("p x (d j e) -> p x j d e", d=d, e=d),
                 axis=AX.XY, op=ALU.add)
 
-        def sums(b, n, i, ms):
-            d = 6 // n
-            six = res[:, b, ms, 14 + 6 * d * i:14 + 6 * d * (i + 1)]
-            nc.vector.tensor_reduce(out=lev[(n, b)][:, ms, n * i:n * (i + 1)],
-                                    in_=six.rearrange("p x (d j e) -> p x j d e", d=d, e=d), axis=AX.XY, op=ALU.add)
+        def total(br):
+            ms = slice(4 * br, 4 * br + 4)
+            nc.vector.tensor_reduce(out=coarse[1][:, ms, 0:1], in_=res[:, 1, ms, 14:50], axis=AX.X, op=ALU.add)
 
-        def total(b, ms):
-            nc.vector.tensor_reduce(out=lev[(1, b)][:, ms, 0:1], in_=lev[(2, b)][:, ms, :], axis=AX.X, op=ALU.add)
+        def store(b, br):
+            nc.sync.dma_start(out=(out_0, out_1)[br][b].rearrange("(p m) j -> p (m j)", m=4),
+                              in_=res[:, b, 4 * br:4 * br + 4, :].rearrange("p m j -> p (m j)"))
 
-        def finish(b, brs):
-            ms = slice(4 * brs[0], 4 * brs[-1] + 4)
-            nc.vector.tensor_tensor(out=res[:, b, ms, 0:14], in0=coarse[b][:, ms, :], in1=fac[:, ms, :], op=ALU.mult)
-            for br in brs:
-                nc.sync.dma_start(out=(out_0, out_1)[br][b].rearrange("(p m) j -> p (m j)", m=4),
-                                  in_=res[:, b, 4 * br:4 * br + 4, :].rearrange("p m j -> p (m j)"))
-
-        def gadd(out, in0, in1):
-            nc.gpsimd.tensor_tensor(out=out, in0=in0, in1=in1, op=ALU.add)
+        def finish(br):
+            ms = slice(4 * br, 4 * br + 4)
+            nc.vector.tensor_tensor(out=res[:, 1, ms, 0:14], in0=coarse[1][:, ms, :], in1=fac[:, ms, :], op=ALU.mult)
+            store(1, br)
 
         def coarse_gpsimd():
+            def add(out, in0, in1):
+                nc.gpsimd.tensor_tensor(out=out, in0=in0, in1=in1, op=ALU.add)
+
             six = res[:, 0, :, 14:50]
-            r3 = six.rearrange("p m (i d w) -> p m i d w", i=3, d=2)
-            r2 = six.rearrange("p m (i d w) -> p m i d w", i=2, d=3)
-            t3 = const.tile([P, NM, 18], F32, name="t3")
-            t2 = const.tile([P, NM, 12], F32, name="t2")
-            u2 = const.tile([P, NM, 4], F32, name="u2")
-            v2 = const.tile([P, NM, 2], F32, name="v2")
-            t2v = t2[:].rearrange("p m (i w) -> p m i w", w=6)
-            gadd(t2v, r2[:, :, :, 0, :], r2[:, :, :, 1, :])
-            gadd(t3[:].rearrange("p m (i w) -> p m i w", w=6), r3[:, :, :, 0, :], r3[:, :, :, 1, :])
-            gadd(t2v, t2v, r2[:, :, :, 2, :])
-            c3 = t3[:].rearrange("p m (j e) -> p m j e", e=2)
-            gadd(lev[(3, 0)], c3[:, :, :, 0], c3[:, :, :, 1])
-            c2 = t2[:].rearrange("p m (j e) -> p m j e", e=3)
-            gadd(u2[:], c2[:, :, :, 0], c2[:, :, :, 1])
-            gadd(lev[(2, 0)], u2[:], c2[:, :, :, 2])
-            gadd(v2[:], coarse[0][:, :, 1:3], coarse[0][:, :, 3:5])
-            gadd(lev[(1, 0)], v2[:, :, 0:1], v2[:, :, 1:2])
+            by3 = six.rearrange("p m (i d w) -> p m i d w", i=3, d=2)
+            by2 = six.rearrange("p m (i d w) -> p m i d w", i=2, d=3)
+            rows3 = const.tile([P, NM, 18], F32, name="rows3")
+            rows2 = const.tile([P, NM, 12], F32, name="rows2")
+            part = const.tile([P, NM, 4], F32, name="part")
+            pair = const.tile([P, NM, 2], F32, name="pair")
+            rows2v = rows2[:].rearrange("p m (i w) -> p m i w", w=6)
+            add(rows2v, by2[:, :, :, 0, :], by2[:, :, :, 1, :])
+            add(rows3[:].rearrange("p m (i w) -> p m i w", w=6), by3[:, :, :, 0, :], by3[:, :, :, 1, :])
+            add(rows2v, rows2v, by2[:, :, :, 2, :])
+            cols3 = rows3[:].rearrange("p m (j e) -> p m j e", e=2)
+            add(coarse[0][:, :, 5:14], cols3[:, :, :, 0], cols3[:, :, :, 1])
+            cols2 = rows2[:].rearrange("p m (j e) -> p m j e", e=3)
+            add(part[:], cols2[:, :, :, 0], cols2[:, :, :, 1])
+            add(coarse[0][:, :, 1:5], part[:], cols2[:, :, :, 2])
+            add(pair[:], coarse[0][:, :, 1:3], coarse[0][:, :, 3:5])
+            add(coarse[0][:, :, 0:1], pair[:, :, 0:1], pair[:, :, 1:2])
             nc.gpsimd.tensor_tensor(out=res[:, 0, :, 0:14], in0=coarse[0][:], in1=fac[:], op=ALU.mult)
             for br in range(2):
-                nc.sync.dma_start(out=(out_0, out_1)[br][0].rearrange("(p m) j -> p (m j)", m=4),
-                                  in_=res[:, 0, 4 * br:4 * br + 4, :].rearrange("p m j -> p (m j)"))
+                store(0, br)
 
         for i in range(WARM):
             dummy()
@@ -314,18 +313,19 @@ def tile_guided_cam_module2_pa_kernel(
         for m in range(NM):
             transposes(m, 0)
             transposes(m, 1)
-            if m >= NM - 3 and m < NM - 1:
-                multiply(0, (2 * (m - (NM - 3)), 2 * (m - (NM - 3)) + 1))
+            if m in (5, 6):
+                for mm in (2 * (m - 5), 2 * (m - 5) + 1):
+                    multiply(0, mm)
             c, g = 1 + m // 4, m % 4
             widen(c, g)
-            empty_w(m, 0, "S")
-            empty_w(m, 1, "S")
+            empty_w(m, 0)
+            empty_w(m, 1)
             if m == 1:
                 quantize_x(0)
             if m > 0:
                 quantize_w(m - 1)
-            if m >= NM - 3:
-                bn_step(m - (NM - 3))
+            if m >= 5:
+                bn_step(m - 5)
             interleave(c, g)
             if m == 4:
                 quantize_x(1)
@@ -334,55 +334,52 @@ def tile_guided_cam_module2_pa_kernel(
             widen(3, g)
             if g == 0:
                 quantize_x(2)
-            if g > 0:
+            else:
                 interleave(3, g - 1)
         interleave(3, G - 1)
-        multiply(1, (0, 1))
-        multiply(1, (2, 3))
-        for j in (2, 3):
-            multiply(0, (2 * j, 2 * j + 1))
-            multiply(1, (2 * j, 2 * j + 1))
-        for c in range(1, NC):
-            per = 512 // CHUNKS[c][1]
-            for j in range(NM // per if c >= 2 else 0):
-                multiply(c, tuple(range(per * j, per * (j + 1))))
-            for i, (r0, r1, cg) in enumerate(G_PIECES):
-                if cg == c - 1:
-                    for m in G_SETS[i]:
-                        for k in PIECES:
-                            if r0 <= k[0] and k[1] <= r1:
-                                pool_half(k[0], k[1], m)
-            if c == 3:
-                coarse_gpsimd()
-            if c == 4:
-                for n, i in ((2, 0), (3, 0), (3, 1)):
-                    sums(1, n, i, slice(0, 8))
+        for m in range(4):
+            multiply(1, m)
+        for m in range(4, NM, 2):
+            for c in (0, 1):
+                multiply(c, m)
+                multiply(c, m + 1)
+        for m in range(NM):
+            bn_relu(0, m)
+            if m == 2:
+                for g in range(G):
+                    widen(4, g)
+                    interleave(4, g)
+            pool(STAGE_ROWS[0][0], STAGE_ROWS[0][1], m)
+            if m == 0:
+                quantize_x(3)
+            if m == 5:
+                quantize_x(4)
+        for s in (1, 2, 3):
             for m in range(NM):
-                bn_relu(c, m)
-                for k in range(len(PIECES)):
-                    if PIECES[k][2] == c and not any(m in G_SETS[i] and G_PIECES[i][0] <= PIECES[k][0] < G_PIECES[i][1] for i in range(3)):
-                        pool(k, m)
-                for i in range(3):
-                    if G_PIECES[i][2] == c and m in G_SETS[i]:
-                        halve(G_PIECES[i][0], G_PIECES[i][1], m)
-                if c == 1 and m == 0:
-                    quantize_x(3)
-                if c == 1 and m == 3:
-                    for g in range(G):
-                        widen(4, g)
-                        if g > 0:
-                            interleave(4, g - 1)
-                    interleave(4, G - 1)
-                if c == 1 and m == 3+1:
-                    quantize_x(4)
-                if c == NC - 1 and m == 4:
-                    sums(1, 2, 1, slice(0, 4))
-                if c == NC - 1 and m == 5:
-                    sums(1, 3, 2, slice(0, 4))
-                if c == NC - 1 and m == 6:
-                    total(1, slice(0, 4))
-        finish(1, (0,))
-        sums(1, 2, 1, slice(4, 8))
-        sums(1, 3, 2, slice(4, 8))
-        total(1, slice(4, 8))
-        finish(1, (1,))
+                multiply(s + 1, m)
+            if s == 2:
+                for m in HALF_TILES:
+                    pool_half(m)
+                coarse_gpsimd()
+            for m in range(NM):
+                bn_relu(s, m)
+                if s == 1 and m in HALF_TILES:
+                    halve(m)
+                else:
+                    pool(STAGE_ROWS[s][0], STAGE_ROWS[s][1], m)
+                if s == 2 and m in (4, 5, 6):
+                    level(*((2, 0, 0), (3, 0, 0), (3, 1, 0))[m - 4])
+                if s == 3 and m in (0, 1, 2):
+                    level(*((2, 0, 1), (3, 0, 1), (3, 1, 1))[m])
+                if s == 3 and m == 4:
+                    level(2, 1, 0)
+                if s == 3 and m == 5:
+                    level(3, 2, 0)
+                if s == 3 and m == 6:
+                    total(0)
+                if s == 3 and m == 7:
+                    finish(0)
+        total(1)
+        level(2, 1, 1)
+        level(3, 2, 1)
+        finish(1)

@@ -82,9 +82,8 @@ def tile_guided_cam_module2_pa_kernel(
             wraw[m] = keep.tile([P, C], BF16, name="wraw%d" % m)
             nc.sync.dma_start(out=wraw[m][:], in_=w.rearrange("(p m) k -> m p k", m=4)[m % 4])
 
-        load_scales(0, 1)
+        load_scales(0, G)
         load_x(0, 0, True)
-        load_scales(1, G)
         for g in range(1, G):
             load_x(0, g, False)
         for m in range(4):
@@ -155,12 +154,12 @@ def tile_guided_cam_module2_pa_kernel(
             junk = psum.tile([P, 512], F32, name="junk", tag="bank")
             nc.tensor.matmul(out=junk[:, 0:DUMMY_N], lhsT=zeros[:, 0:P], rhs=zeros[:], start=True, stop=True)
 
-        def widen(u, g):
+        def widen(u, g, ts=(0, 1, 2, 3)):
             f0, width = UNITS[u]
-            if g == 0:
+            if u not in xw:
                 xw[u] = keep.tile([P, G, 4, width], BF16, name="xw%d" % u)
             b, n0 = divmod(f0, HW)
-            for t in range(4):
+            for t in ts:
                 dst = xw[u][:, g, t, :]
                 src = xb[(b, g)][:, t, n0:n0 + width].bitcast(FP8)
                 if (u, g) in V_WIDEN or (u == 0 and t >= 2):
@@ -307,6 +306,7 @@ def tile_guided_cam_module2_pa_kernel(
             dummy()
         for g in range(G):
             widen(0, g)
+            widen(1, 0, (g,))
             if g > 0:
                 interleave(0, g - 1)
         interleave(0, G - 1)
@@ -317,7 +317,8 @@ def tile_guided_cam_module2_pa_kernel(
                 for mm in (2 * (m - 5), 2 * (m - 5) + 1):
                     multiply(0, mm)
             c, g = 1 + m // 4, m % 4
-            widen(c, g)
+            if m > 0:
+                widen(c, g)
             empty_w(m, 0)
             empty_w(m, 1)
             if m == 1:

@@ -313,9 +313,8 @@ def tile_guided_cam_module2_pa_kernel(
         for m in range(NM):
             transposes(m, 0)
             transposes(m, 1)
-            if m in (5, 6):
-                for mm in (2 * (m - 5), 2 * (m - 5) + 1):
-                    multiply(0, mm)
+            for cc, mm in {4: ((0, 0), (0, 1),), 5: ((0, 2), (0, 3),)}.get(m, ()):
+                multiply(cc, mm)
             c, g = 1 + m // 4, m % 4
             if m > 0:
                 widen(c, g)
@@ -338,22 +337,18 @@ def tile_guided_cam_module2_pa_kernel(
             else:
                 interleave(3, g - 1)
         interleave(3, G - 1)
-        for m in range(4):
-            multiply(1, m)
-        for m in range(4, NM, 2):
-            for c in (0, 1):
-                multiply(c, m)
-                multiply(c, m + 1)
+        for cc, mm in ((1, 0), (1, 1), (1, 2), (1, 3), (0, 4), (0, 5), (1, 4), (1, 5), (0, 6), (0, 7), (1, 6), (1, 7),):
+            multiply(cc, mm)
         for m in range(NM):
             bn_relu(0, m)
-            if m == 2:
+            if m == 4:
                 for g in range(G):
                     widen(4, g)
                     interleave(4, g)
             pool(STAGE_ROWS[0][0], STAGE_ROWS[0][1], m)
             if m == 0:
                 quantize_x(3)
-            if m == 5:
+            if m == 7:
                 quantize_x(4)
         for s in (1, 2, 3):
             for m in range(NM):

from contextlib import ExitStack

import concourse.mybir as mybir
from concourse.masks import make_identity

F32 = mybir.dt.float32
BF16 = mybir.dt.bfloat16
U32 = mybir.dt.uint32
U8 = mybir.dt.uint8
FP8 = mybir.dt.float8_e4m3fn
FP8X4 = mybir.dt.float8_e4m3fn_x4
ACT = mybir.ActivationFunctionType
ALU = mybir.AluOpType
AX = mybir.AxisListType

B, C, CO, HW = 2, 2048, 512, 576
EPS = 1e-5
P = 128
G = 4
NM = 8
COLS = B * HW

CHUNKS = ((0, 256), (256, 256), (512, 256), (768, 256), (1024, 128))
UNITS = ((0, 256), (256, 320), (576, 192), (768, 256), (1024, 128))
V_WIDEN = ((1, 1), (1, 3), (2, 3), (3, 3))
STAGES = ((0, 512), (512, 256), (768, 256), (1024, 128))
STAGE_ROWS = ((0, 5), (5, 8), (8, 10), (10, 12))
HALF_ROWS = (5, 8)
HALF_TILES = (2, 3, 4, 5)
WARM = 3
DUMMY_N = 256

FLOPS = 2 * 2 * CO * C * COLS


def tile_guided_cam_module2_pa_kernel(
    tc, x_bytes, x_scale, wq, q_scale, q_bias, q_mean, q_var,
    wk, k_scale, k_bias, k_mean, k_var, out_0, out_1,
):
    nc = tc.nc
    with ExitStack() as ctx:
        const = ctx.enter_context(tc.tile_pool(name="const", bufs=1))
        keep = ctx.enter_context(tc.tile_pool(name="keep", bufs=1))
        xgp = ctx.enter_context(tc.tile_pool(name="xgp", bufs=3))
        wgp = ctx.enter_context(tc.tile_pool(name="wgp", bufs=3))
        psum = ctx.enter_context(tc.psum_pool(name="psum", bufs=8))
        ctx.enter_context(tc.manual_schedule())

        zeros = const.tile([P, DUMMY_N], F32, name="zeros")
        nc.vector.memset(zeros[:], 0.0)
        ident = const.tile([P, P], F32, name="ident")
        make_identity(nc, ident[:])

        bn_in = const.tile([P, 8, 16], BF16, name="bn_in")
        bn_vecs = (q_scale, k_scale, q_bias, k_bias, q_mean, k_mean, q_var, k_var)

        def load_bn(i, queue):
            queue.dma_start(out=bn_in[:, i, 0:4], in_=bn_vecs[i].rearrange("(p m) -> p m", m=4))

        load_bn(6, nc.scalar)
        load_bn(7, nc.scalar)
        warm = const.tile([P, 1], F32, name="warm")
        nc.scalar.activation(out=warm[:], in_=zeros[:, 0:1], func=ACT.Relu)

        xs = const.tile([P, G, 8], F32, name="xs")
        scales = x_scale[0].rearrange("(g p t) a b -> p g (t a b)", p=P, t=4)

        def load_scales(g0, g1):
            nc.sync.dma_start(out=xs[:, g0:g1, 0:4], in_=scales[:, g0:g1, :])

        xb = {}
        wraw = {}

        def load_x(b, g, halves):
            xb[(b, g)] = keep.tile([P, 4, HW], U8, name="xb%d%d" % (b, g))
            src = x_bytes[b].rearrange("(g p t) h w -> g p t (h w)", p=P, t=4)[g]
            for t0, t1 in ((0, 2), (2, 4)) if halves else ((0, 4),):
                nc.sync.dma_start(out=xb[(b, g)][:, t0:t1, :], in_=src[:, t0:t1, :])

        def load_w(m):
            w = wq if m < 4 else wk
            wraw[m] = keep.tile([P, C], BF16, name="wraw%d" % m)
            nc.sync.dma_start(out=wraw[m][:], in_=w.rearrange("(p m) k -> m p k", m=4)[m % 4])

        load_scales(0, G)
        load_x(0, 0, True)
        for g in range(1, G):
            load_x(0, g, False)
        for m in range(4):
            load_w(m)
            if m >= 2:
                load_bn(m - 2, nc.sync)
        for g in range(G):
            load_w(4 + g)
            if g < 2:
                load_bn(4 + g, nc.sync)
            load_x(1, g, False)
            if g < 2:
                load_bn(2 + g, nc.sync)

        fac = const.tile([P, NM, 14], F32, name="fac")
        nc.gpsimd.memset(fac[:], 1.0)
        for first, end, factor in ((0, 1, 1.0 / 36.0), (1, 5, 1.0 / 9.0), (5, 14, 0.25)):
            nc.gpsimd.tensor_scalar(out=fac[:, :, first:end], in0=fac[:, :, first:end], scalar1=factor, scalar2=0.0,
                                    op0=ALU.mult, op1=ALU.add)

        def both(t):
            return t[:].rearrange("p (b m) -> p b m", b=2)

        expo = const.tile([P, NM], F32, name="expo")
        nc.gpsimd.memset(expo[:], -0.5)
        vare = const.tile([P, NM], F32, name="vare")
        nc.gpsimd.tensor_scalar(out=both(vare), in0=bn_in[:, 6:8, 0:4], scalar1=1.0, scalar2=EPS, op0=ALU.mult, op1=ALU.add)
        inv = const.tile([P, NM], F32, name="inv")
        nc.gpsimd.tensor_tensor(out=inv[:], in0=vare[:], in1=expo[:], op=ALU.pow)
        bn_a = const.tile([P, NM], F32, name="bn_a")
        ma = const.tile([P, NM], F32, name="ma")
        bn_b = const.tile([P, NM], F32, name="bn_b")

        def bn_step(i):
            if i == 0:
                nc.vector.scalar_tensor_tensor(out=both(bn_a), in0=bn_in[:, 0:2, 0:4], scalar=0.0625, in1=both(inv),
                                               op0=ALU.mult, op1=ALU.mult)
            elif i == 1:
                nc.vector.tensor_tensor(out=both(ma), in0=bn_in[:, 4:6, 0:4], in1=both(bn_a), op=ALU.mult)
            else:
                nc.vector.scalar_tensor_tensor(out=both(bn_b), in0=bn_in[:, 2:4, 0:4], scalar=0.0625, in1=both(ma),
                                               op0=ALU.mult, op1=ALU.subtract)

        res = const.tile([P, B, NM, 50], F32, name="res")
        coarse = {}
        for b in range(B):
            coarse[b] = const.tile([P, NM, 14], F32, name="coarse%d" % b)
        FIRST = {1: 0, 2: 1, 3: 5}
        z = {}
        half = {}
        for m in range(NM):
            z[m] = keep.tile([P, COLS], F32, name="z%d" % m)
            if m in HALF_TILES:
                half[m] = keep.tile([P, 48 * (HALF_ROWS[1] - HALF_ROWS[0])], F32, name="half%d" % m)

        xw = {}
        xg = {}
        xc = {}
        xsc = {}
        wg = {}
        wbank = {}
        wc = {}
        wsc = {}
        acc = {}
        sums_bank = {}

        def dummy():
            junk = psum.tile([P, 512], F32, name="junk", tag="bank")
            nc.tensor.matmul(out=junk[:, 0:DUMMY_N], lhsT=zeros[:, 0:P], rhs=zeros[:], start=True, stop=True)

        def widen(u, g, ts=(0, 1, 2, 3)):
            f0, width = UNITS[u]
            if u not in xw:
                xw[u] = keep.tile([P, G, 4, width], BF16, name="xw%d" % u)
            b, n0 = divmod(f0, HW)
            for t in ts:
                dst = xw[u][:, g, t, :]
                src = xb[(b, g)][:, t, n0:n0 + width].bitcast(FP8)
                if (u, g) in V_WIDEN or (u == 0 and t >= 2):
                    nc.vector.tensor_scalar(out=dst, in0=src, scalar1=xs[:, g, t:t + 1], scalar2=None, op0=ALU.mult)
                else:
                    nc.scalar.activation(out=dst, in_=src, func=ACT.Copy, scale=xs[:, g, t:t + 1])

        def interleave(c, g):
            f0, width = CHUNKS[c]
            if g == 0:
                xg[c] = xgp.tile([P, G * width * 4], BF16, name="xg", tag="xg", align_bytes=64)
            for u, (u0, uw) in enumerate(UNITS):
                a, b = max(f0, u0), min(f0 + width, u0 + uw)
                if a < b:
                    dst = xg[c][:, 4 * (g * width + a - f0):4 * (g * width + b - f0)]
                    src = xw[u][:, g, :, a - u0:b - u0]
                    if c == len(CHUNKS) - 1:
                        nc.gpsimd.tensor_scalar(out=dst.rearrange("p (n t) -> p n t", t=4), in0=src.rearrange("p t n -> p n t"),
                                                scalar1=1.0, scalar2=0.0, op0=ALU.mult, op1=ALU.add)
                    else:
                        nc.vector.tensor_copy(out=dst.rearrange("p (n i t) -> p n t i", i=4, t=4),
                                              in_=src.rearrange("p t (n i) -> p n t i", i=4))

        def quantize_x(c):
            width = CHUNKS[c][1]
            xc[c] = keep.tile([P, G * width], U32, name="xc%d" % c, align_bytes=64)
            xsc[c] = keep.tile([P, G * width], U8, name="xsc%d" % c, align_bytes=64)
            nc.vector.quantize_mx(out=xc[c][:].bitcast(FP8X4), scales=xsc[c][:], in_=xg[c][:])

        def transposes(m, h):
            words = wraw[m][:].bitcast(F32)
            wbank[(m, h)] = psum.tile([P, 512], F32, name="wbank", tag="bank")
            for gg in range(2):
                g = 2 * h + gg
                for u in range(2):
                    nc.tensor.transpose(wbank[(m, h)][:, (2 * gg + u) * P:(2 * gg + u + 1) * P],
                                        words[:, 256 * g + u:256 * (g + 1):2], ident[:])

        def empty_w(m, h):
            if h == 0:
                wg[m] = wgp.tile([P, G * P * 4], BF16, name="wg", tag="wg", align_bytes=64)
            nc.scalar.copy(
                out=wg[m][:].bitcast(F32)[:, 512 * h:512 * (h + 1)].rearrange("p (g r u) -> p g r u", g=2, u=2),
                in_=wbank[(m, h)][:].rearrange("p (g u r) -> p g r u", g=2, u=2))

        def quantize_w(m):
            wc[m] = keep.tile([P, G * P], U32, name="wc%d" % m, align_bytes=64)
            wsc[m] = keep.tile([P, G * P], U8, name="wsc%d" % m, align_bytes=64)
            nc.vector.quantize_mx(out=wc[m][:].bitcast(FP8X4), scales=wsc[m][:], in_=wg[m][:])

        def multiply(c, m):
            f0, width = CHUNKS[c]
            bank, col = (("pair", m), f0) if c < 2 else ((c, m * width // 512), m * width % 512)
            if bank not in sums_bank:
                sums_bank[bank] = psum.tile([P, 512], F32, name="sums", tag="bank")
            acc[(c, m)] = sums_bank[bank][:, col:col + width]
            for g in range(G):
                nc.tensor.matmul_mx(
                    out=acc[(c, m)],
                    lhsT=wc[m][:, g * P:(g + 1) * P].bitcast(FP8X4),
                    lhsT_scale=wsc[m][:, g * P:(g + 1) * P],
                    rhs=xc[c][:, g * width:(g + 1) * width].bitcast(FP8X4),
                    rhs_scale=xsc[c][:, g * width:(g + 1) * width],
                    start=(g == 0), stop=(g == G - 1))

        def bn_relu(s, m):
            f0, width = STAGES[s]
            src = sums_bank[("pair", m)][:] if s == 0 else acc[(s + 1, m)]
            nc.scalar.activation(out=z[m][:, f0:f0 + width], in_=src, func=ACT.Relu,
                                 bias=bn_b[:, m:m + 1], scale=bn_a[:, m:m + 1])

        def by_batch(r0, r1):
            return [(max(r0, 6 * b), min(r1, 6 * b + 6)) for b in range(B) if max(r0, 6 * b) < min(r1, 6 * b + 6)]

        def means_6x6(r0, r1, m):
            b = r0 // 6
            return res[:, b, m, 14 + 6 * (r0 - 6 * b):14 + 6 * (r1 - 6 * b)].rearrange("p (r w) -> p r w", w=6)

        def pool(r0, r1, m):
            for a, e in by_batch(r0, r1):
                nc.vector.tensor_reduce(out=means_6x6(a, e, m),
                                        in_=z[m][:, 96 * a:96 * e].rearrange("p (r i w j) -> p r w i j", i=4, w=6, j=4),
                                        axis=AX.XY, op=ALU.add)

        def halve(m):
            rows = z[m][:, 96 * HALF_ROWS[0]:96 * HALF_ROWS[1]].rearrange("p (r h q) -> p r h q", h=2, q=48)
            nc.gpsimd.tensor_tensor(out=half[m][:].rearrange("p (r q) -> p r q", q=48),
                                    in0=rows[:, :, 0, :], in1=rows[:, :, 1, :], op=ALU.add)

        def pool_half(m):
            for a, e in by_batch(*HALF_ROWS):
                src = half[m][:, 48 * (a - HALF_ROWS[0]):48 * (e - HALF_ROWS[0])]
                nc.vector.tensor_reduce(out=means_6x6(a, e, m), in_=src.rearrange("p (r i w j) -> p r w i j", i=2, w=6, j=4),
                                        axis=AX.XY, op=ALU.add)

        def level(n, i, br):
            d = 6 // n
            ms = slice(4 * br, 4 * br + 4)
            nc.vector.tensor_reduce(
                out=coarse[1][:, ms, FIRST[n] + n * i:FIRST[n] + n * (i + 1)],
                in_=res[:, 1, ms, 14 + 6 * d * i:14 + 6 * d * (i + 1)].rearrange("p x (d j e) -> p x j d e", d=d, e=d),
                axis=AX.XY, op=ALU.add)

        def total(br):
            ms = slice(4 * br, 4 * br + 4)
            nc.vector.tensor_reduce(out=coarse[1][:, ms, 0:1], in_=res[:, 1, ms, 14:50], axis=AX.X, op=ALU.add)

        def store(b, br):
            nc.sync.dma_start(out=(out_0, out_1)[br][b].rearrange("(p m) j -> p (m j)", m=4),
                              in_=res[:, b, 4 * br:4 * br + 4, :].rearrange("p m j -> p (m j)"))

        def finish(br):
            ms = slice(4 * br, 4 * br + 4)
            nc.vector.tensor_tensor(out=res[:, 1, ms, 0:14], in0=coarse[1][:, ms, :], in1=fac[:, ms, :], op=ALU.mult)
            store(1, br)

        def coarse_gpsimd():
            def add(out, in0, in1):
                nc.gpsimd.tensor_tensor(out=out, in0=in0, in1=in1, op=ALU.add)

            six = res[:, 0, :, 14:50]
            by3 = six.rearrange("p m (i d w) -> p m i d w", i=3, d=2)
            by2 = six.rearrange("p m (i d w) -> p m i d w", i=2, d=3)
            rows3 = const.tile([P, NM, 18], F32, name="rows3")
            rows2 = const.tile([P, NM, 12], F32, name="rows2")
            part = const.tile([P, NM, 4], F32, name="part")
            pair = const.tile([P, NM, 2], F32, name="pair")
            rows2v = rows2[:].rearrange("p m (i w) -> p m i w", w=6)
            add(rows2v, by2[:, :, :, 0, :], by2[:, :, :, 1, :])
            add(rows3[:].rearrange("p m (i w) -> p m i w", w=6), by3[:, :, :, 0, :], by3[:, :, :, 1, :])
            add(rows2v, rows2v, by2[:, :, :, 2, :])
            cols3 = rows3[:].rearrange("p m (j e) -> p m j e", e=2)
            add(coarse[0][:, :, 5:14], cols3[:, :, :, 0], cols3[:, :, :, 1])
            cols2 = rows2[:].rearrange("p m (j e) -> p m j e", e=3)
            add(part[:], cols2[:, :, :, 0], cols2[:, :, :, 1])
            add(coarse[0][:, :, 1:5], part[:], cols2[:, :, :, 2])
            add(pair[:], coarse[0][:, :, 1:3], coarse[0][:, :, 3:5])
            add(coarse[0][:, :, 0:1], pair[:, :, 0:1], pair[:, :, 1:2])
            nc.gpsimd.tensor_tensor(out=res[:, 0, :, 0:14], in0=coarse[0][:], in1=fac[:], op=ALU.mult)
            for br in range(2):
                store(0, br)

        for i in range(WARM):
            dummy()
        for g in range(G):
            widen(0, g)
            widen(1, 0, (g,))
            if g > 0:
                interleave(0, g - 1)
        interleave(0, G - 1)
        for m in range(NM):
            transposes(m, 0)
            transposes(m, 1)
            for cc, mm in {4: ((0, 0), (0, 1),), 5: ((0, 2), (0, 3),)}.get(m, ()):
                multiply(cc, mm)
            c, g = 1 + m // 4, m % 4
            if m > 0:
                widen(c, g)
            empty_w(m, 0)
            empty_w(m, 1)
            if m == 1:
                quantize_x(0)
            if m > 0:
                quantize_w(m - 1)
            if m >= 5:
                bn_step(m - 5)
            interleave(c, g)
            if m == 4:
                quantize_x(1)
        quantize_w(NM - 1)
        for g in range(G):
            widen(3, g)
            if g == 0:
                quantize_x(2)
            else:
                interleave(3, g - 1)
        interleave(3, G - 1)
        for cc, mm in ((1, 0), (1, 1), (1, 2), (1, 3), (0, 4), (0, 5), (1, 4), (1, 5), (0, 6), (0, 7), (1, 6), (1, 7),):
            multiply(cc, mm)
        for m in range(NM):
            bn_relu(0, m)
            if m == 4:
                for g in range(G):
                    widen(4, g)
                    interleave(4, g)
            pool(STAGE_ROWS[0][0], STAGE_ROWS[0][1], m)
            if m == 0:
                quantize_x(3)
            if m == 7:
                quantize_x(4)
        for s in (1, 2, 3):
            for m in range(NM):
                multiply(s + 1, m)
            if s == 2:
                for m in HALF_TILES:
                    pool_half(m)
                coarse_gpsimd()
            for m in range(NM):
                bn_relu(s, m)
                if s == 1 and m in HALF_TILES:
                    halve(m)
                else:
                    pool(STAGE_ROWS[s][0], STAGE_ROWS[s][1], m)
                if s == 2 and m in (4, 5, 6):
                    level(*((2, 0, 0), (3, 0, 0), (3, 1, 0))[m - 4])
                if s == 3 and m in (0, 1, 2):
                    level(*((2, 0, 1), (3, 0, 1), (3, 1, 1))[m])
                if s == 3 and m == 4:
                    level(2, 1, 0)
                if s == 3 and m == 5:
                    level(3, 2, 0)
                if s == 3 and m == 6:
                    total(0)
                if s == 3 and m == 7:
                    finish(0)
        total(1)
        level(2, 1, 1)
        level(3, 2, 1)
        finish(1)
